import numpy as np
import ml_dtypes


def mxq(x, axis, fmt="e4m3"):
    dtype, down = {"e4m3": (ml_dtypes.float8_e4m3fn, 7), "e5m2": (ml_dtypes.float8_e5m2, 14)}[fmt]
    v = np.moveaxis(np.asarray(x, np.float32).astype(ml_dtypes.bfloat16).astype(np.float64), axis, -1)
    blocks = v.reshape(v.shape[:-1] + (-1, 32))
    amax = np.abs(blocks).max(-1, keepdims=True)
    byte = np.maximum(np.where(amax > 0, np.frexp(amax)[1] - 1 + 127, 0) - down, 1)
    scale = np.exp2(byte - 127.0)
    codes = (blocks / scale).astype(np.float32).astype(dtype).astype(np.float64)
    return np.moveaxis((codes * scale).reshape(v.shape), -1, axis)


WIDE = False


def mx_kscale(k):
    if not WIDE:
        return np.ones(k)
    levels = np.array([10, -10, 5, -5, 0])
    if k % 512:
        return np.exp2(np.random.permutation(np.resize(levels, k // 32))).repeat(32)
    a = np.empty((k // 512, 16))
    for p in range(k // 512):
        a[p, :8] = np.random.permutation(np.resize(levels, 8))
        for g in range(8):
            far = levels[np.abs(levels - a[p, g]) >= 10]
            a[p, g + 8] = far[np.random.randint(len(far))]
    return np.exp2(a.ravel()).repeat(32)


BF16 = ml_dtypes.bfloat16


def bf(x):
    return np.asarray(x, np.float32).astype(BF16)


def f64(x):
    return np.asarray(x).astype(np.float64)


B, S, DIM, H, KV, HD = 1, 512, 2048, 16, 4, 128
ROPE_THETA = 10000.0


def rope_tables():
    inv_freq = 1.0 / ROPE_THETA ** (np.arange(0, HD, 2) / HD)
    freqs = np.outer(np.arange(S), inv_freq)
    return np.cos(freqs), np.sin(freqs)


def rot(t, cos, sin):
    te, to = t[..., 0::2], t[..., 1::2]
    re = te * cos - to * sin
    ro = te * sin + to * cos
    return np.stack((re, ro), axis=-1).reshape(t.shape)


def draw0():
    s = mx_kscale(DIM)
    c, sn = rope_tables()
    return {"x": bf(np.random.standard_normal((B, S, DIM)) * s),
            "wq": bf(np.random.standard_normal((DIM, H * HD)) / np.sqrt(DIM) / s[:, None]),
            "wk": bf(np.random.standard_normal((DIM, KV * HD)) / np.sqrt(DIM) / s[:, None]),
            "wv": bf(np.random.standard_normal((DIM, KV * HD)) / np.sqrt(DIM) / s[:, None]),
            "freqs_cos": bf(c), "freqs_sin": bf(sn)}


def core(x, wq, wk, wv, freqs_cos, freqs_sin):
    xq = mxq(f64(x), 2, "e4m3")
    q = (xq @ mxq(f64(wq), 0, "e4m3")).reshape(B, S, H, HD)
    k = (xq @ mxq(f64(wk), 0, "e4m3")).reshape(B, S, KV, HD)
    v = (xq @ mxq(f64(wv), 0, "e4m3")).reshape(B, S, KV, HD)
    cos = f64(freqs_cos)[:S][None, :, None, :]
    sin = f64(freqs_sin)[:S][None, :, None, :]
    return rot(q, cos, sin), rot(k, cos, sin), v


def e4m3fn_bytes(y):
    return np.clip(np.asarray(y, np.float64), -448.0, 448.0).astype(np.float32).astype(ml_dtypes.float8_e4m3fn).view(np.uint8)


def e4m3fn_values(b):
    return np.asarray(b, np.uint8).view(ml_dtypes.float8_e4m3fn).astype(np.float64)


def setup_inputs():
    d = draw0()
    x0 = np.asarray(d['wq']).astype(np.float64)
    s = (np.max(np.abs(x0), axis=(1,), keepdims=True) / 448.0).astype(np.float32)
    out = {}
    for k, v in d.items():
        if k == 'wq':
            out['wq_bytes'] = e4m3fn_bytes(x0 / s.astype(np.float64))
            out['wq_scale'] = s
        else:
            out[k] = v
    return out


def reference(x, wq_bytes, wq_scale, wk, wv, freqs_cos, freqs_sin):
    return core(x, e4m3fn_values(wq_bytes) * wq_scale.astype(np.float64), wk, wv, freqs_cos, freqs_sin)

@@ -1,0 +1,280 @@
+from contextlib import ExitStack
+
+import concourse.mybir as mybir
+from concourse.masks import make_identity
+
+F32 = mybir.dt.float32
+BF16 = mybir.dt.bfloat16
+U32 = mybir.dt.uint32
+U8 = mybir.dt.uint8
+FP8 = mybir.dt.float8_e4m3fn
+FP8X4 = mybir.dt.float8_e4m3fn_x4
+MULT = mybir.AluOpType.mult
+ADD = mybir.AluOpType.add
+COPY = mybir.ActivationFunctionType.Copy
+
+P = 128
+PACK = 4
+TOKENS = 512
+DIM = 2048
+PASSES = 4
+NCH = 512
+ROW_TILES = 4
+HD = 128
+
+FLOPS = 2 * TOKENS * DIM * (2048 + 512 + 512)
+
+MANUAL = False
+ON_SCALAR = {0: (), 1: (2, 3), 2: (3,), 3: (2, 3), 4: (3,), 5: (0, 1, 2, 3)}
+
+
+def tile_attention_pa_kernel(
+    tc, x, wq_bytes, wq_scale, wk, wv, freqs_cos, freqs_sin, out_0, out_1, out_2
+):
+    nc = tc.nc
+    x_rows = x.rearrange("b s k -> (b s) k")
+    wq_view = wq_bytes.rearrange("(g p t) n -> g p t n", p=P, t=PACK)
+    wk_view = wk.rearrange("(g p t) n -> g p t n", p=P, t=PACK)
+    wv_view = wv.rearrange("(g p t) n -> g p t n", p=P, t=PACK)
+    q_out = out_0.rearrange("b s h d -> (b s) (h d)")
+    k_out = out_1.rearrange("b s h d -> (b s) (h d)")
+    v_out = out_2.rearrange("b s h d -> (b s) (h d)")
+
+    with ExitStack() as ctx:
+        const = ctx.enter_context(tc.tile_pool(name="const", bufs=1))
+        raw = ctx.enter_context(tc.tile_pool(name="raw", bufs=1))
+        keep = ctx.enter_context(tc.tile_pool(name="keep", bufs=1))
+        work = ctx.enter_context(tc.tile_pool(name="work", bufs=2))
+        psum = ctx.enter_context(tc.psum_pool(name="psum", bufs=8))
+        if MANUAL:
+            ctx.enter_context(tc.manual_schedule())
+
+        wsc = const.tile([P, PASSES, PACK], F32, name="wsc", tag="wsc")
+        nc.scalar.dma_start(out=wsc[:], in_=wq_scale.rearrange("(g p t) o -> p g (t o)", p=P, t=PACK))
+        cos_t = const.tile([P, ROW_TILES, HD // 2], BF16, name="cos_t", tag="cos_t")
+        nc.scalar.dma_start(out=cos_t[:], in_=freqs_cos.rearrange("(m p) i -> p m i", p=P))
+        sin_t = const.tile([P, ROW_TILES, HD // 2], BF16, name="sin_t", tag="sin_t")
+        nc.scalar.dma_start(out=sin_t[:], in_=freqs_sin.rearrange("(m p) i -> p m i", p=P))
+
+        wq_b = {}
+        wkv_raw = {}
+        x_raw = {}
+
+        def load_wq(j, g):
+            t = raw.tile([P, PACK, NCH], U8, name="wqb%d_%d" % (j, g), tag="wqb%d_%d" % (j, g))
+            nc.sync.dma_start(out=t[:], in_=wq_view[g, :, :, j * NCH : (j + 1) * NCH])
+            wq_b[(j + 1, g)] = t
+
+        def load_kv(c, g):
+            view = wk_view if c == 0 else wv_view
+            t = raw.tile([P, PACK, NCH], BF16, name="wkv%d_%d" % (c, g), tag="wkv%d_%d" % (c, g))
+            nc.sync.dma_start(out=t[:], in_=view[g])
+            wkv_raw[(c, g)] = t
+
+        def load_x(m):
+            t = work.tile([P, DIM], BF16, name="xraw%d" % m, tag="plane", bufs=8)
+            nc.sync.dma_start(out=t[:], in_=x_rows[m * P : (m + 1) * P, :])
+            x_raw[m] = t
+
+        load_wq(0, 0)
+        load_kv(0, 0)
+        load_x(0)
+        load_x(1)
+        load_kv(0, 1)
+        load_wq(0, 1)
+        load_x(2)
+        load_kv(0, 2)
+        load_x(3)
+        load_wq(0, 2)
+        load_kv(0, 3)
+        load_wq(0, 3)
+        for j in range(1, 4):
+            for g in range(PASSES):
+                load_wq(j, g)
+        for g in range(PASSES):
+            load_kv(5, g)
+
+        ident = const.tile([P, P], F32, name="ident", tag="ident")
+        make_identity(nc, ident[:])
+        warm = const.tile([P, 2], F32, name="warm", tag="warm")
+        nc.vector.memset(warm[:, 0:1], 0.0)
+        nc.scalar.activation(out=warm[:, 1:2], in_=warm[:, 0:1], func=COPY)
+
+        cos2 = const.tile([P, ROW_TILES, HD], F32, name="cos2", tag="cos2")
+        sin2 = const.tile([P, ROW_TILES, HD], F32, name="sin2", tag="sin2")
+        cos_flat = cos_t[:].rearrange("p m i -> p (m i)")
+        sin_flat = sin_t[:].rearrange("p m i -> p (m i)")
+        cos2_v = cos2[:].rearrange("p m (i e) -> p (m i) e", e=2)
+        sin2_v = sin2[:].rearrange("p m (i e) -> p (m i) e", e=2)
+        nc.vector.tensor_copy(out=cos2_v[:, :, 0], in_=cos_flat)
+        nc.vector.tensor_copy(out=cos2_v[:, :, 1], in_=cos_flat)
+        nc.vector.tensor_copy(out=sin2_v[:, :, 0], in_=sin_flat)
+        nc.vector.tensor_scalar_mul(out=sin2_v[:, :, 1], in0=sin_flat, scalar1=-1.0)
+
+        x_codes = keep.tile([P, ROW_TILES, PASSES * P], U32, name="x_codes", tag="x_codes", align_bytes=64)
+        x_scales = keep.tile([P, ROW_TILES, PASSES * P], U8, name="x_scales", tag="x_scales", align_bytes=64)
+        w_codes = {}
+        w_scales = {}
+        for c in range(6):
+            w_codes[c] = keep.tile([P, PASSES, NCH], U32, name="w_codes%d" % c, tag="w_codes%d" % c, align_bytes=64)
+            w_scales[c] = keep.tile([P, PASSES, NCH], U8, name="w_scales%d" % c, tag="w_scales%d" % c, align_bytes=64)
+
+        planes = {}
+        grouped = {}
+        x_banks = {}
+        x_grouped = {}
+        acc = {}
+        prod = {}
+
+        def transpose_x(m):
+            words = x_raw[m][:].bitcast(F32)
+            for h in range(2):
+                bank = psum.tile([P, 512], F32, name="xt%d_%d" % (m, h), tag="bank")
+                for gl in range(2):
+                    g = 2 * h + gl
+                    for u in range(2):
+                        col = (2 * gl + u) * P
+                        nc.tensor.transpose(bank[:, col : col + P], words[:, 256 * g + u : 256 * (g + 1) : 2], ident[:])
+                x_banks[(m, h)] = bank
+
+        def copy_x(m):
+            xg = work.tile([P, DIM], BF16, name="xg%d" % m, tag="xg", bufs=2, align_bytes=64)
+            xg_words = xg[:].bitcast(F32)
+            for h in range(2):
+                nc.scalar.copy(
+                    out=xg_words[:, 512 * h : 512 * (h + 1)].rearrange("p (g r u) -> p g r u", g=2, u=2),
+                    in_=x_banks[(m, h)][:].rearrange("p (g u r) -> p g r u", g=2, u=2),
+                )
+            x_grouped[m] = xg
+
+        def quantize_x(m):
+            nc.vector.quantize_mx(out=x_codes[:, m, :].bitcast(FP8X4), scales=x_scales[:, m, :], in_=x_grouped[m][:])
+
+        def widen(c, g):
+            pl = work.tile([P, PACK, NCH], BF16, name="pl%d_%d" % (c, g), tag="plane", bufs=8)
+            for t in range(PACK):
+                nc.scalar.activation(
+                    out=pl[:, t, :], in_=wq_b[(c, g)][:, t, :].bitcast(FP8), func=COPY, scale=wsc[:, g, t : t + 1]
+                )
+            planes[(c, g)] = pl
+
+        def interleave(c, g):
+            src = planes[(c, g)] if 1 <= c <= 4 else wkv_raw[(c, g)]
+            gr = work.tile([P, PACK * NCH], BF16, name="gr%d_%d" % (c, g), tag="gr", bufs=6, align_bytes=64)
+            dst_v = gr[:].rearrange("p (n t) -> p n t", t=PACK)
+            src_v = src[:].rearrange("p t n -> p n t")
+            if g in ON_SCALAR[c]:
+                nc.scalar.copy(out=dst_v, in_=src_v)
+            else:
+                nc.vector.tensor_copy(out=dst_v, in_=src_v)
+            grouped[(c, g)] = gr
+
+        def quantize_w(c, g):
+            nc.vector.quantize_mx(
+                out=w_codes[c][:, g, :].bitcast(FP8X4), scales=w_scales[c][:, g, :], in_=grouped[(c, g)][:]
+            )
+
+        def multiply(c, g):
+            for m in range(ROW_TILES):
+                if g == 0:
+                    acc[(c, m)] = psum.tile([P, NCH], F32, name="acc%d_%d" % (c, m), tag="bank")
+                nc.tensor.matmul_mx(
+                    out=acc[(c, m)][:],
+                    lhsT=x_codes[:, m, g * P : (g + 1) * P].bitcast(FP8X4),
+                    lhsT_scale=x_scales[:, m, g * P : (g + 1) * P],
+                    rhs=w_codes[c][:, g, :].bitcast(FP8X4),
+                    rhs_scale=w_scales[c][:, g, :],
+                    start=(g == 0),
+                    stop=(g == PASSES - 1),
+                )
+
+        def store(c, m, tile_ap):
+            rows = slice(m * P, (m + 1) * P)
+            if c == 0:
+                dst = k_out[rows, :]
+            elif c == 5:
+                dst = v_out[rows, :]
+            else:
+                dst = q_out[rows, (c - 1) * NCH : c * NCH]
+            nc.sync.dma_start(out=dst, in_=tile_ap)
+
+        def rope_mul(c, m):
+            bank_v = acc[(c, m)][:].rearrange("p (h d) -> p h d", d=HD)
+            t1 = work.tile([P, NCH], F32, name="t1_%d_%d" % (c, m), tag="t1", bufs=3)
+            t2 = work.tile([P, NCH], F32, name="t2_%d_%d" % (c, m), tag="t2", bufs=3)
+            shape = [P, NCH // HD, HD]
+            nc.vector.tensor_tensor(
+                out=t1[:].rearrange("p (h d) -> p h d", d=HD),
+                in0=bank_v,
+                in1=cos2[:, m, :].unsqueeze(1).to_broadcast(shape),
+                op=MULT,
+            )
+            nc.vector.tensor_tensor(
+                out=t2[:].rearrange("p (h d) -> p h d", d=HD),
+                in0=bank_v,
+                in1=sin2[:, m, :].unsqueeze(1).to_broadcast(shape),
+                op=MULT,
+            )
+            prod[(c, m)] = (t1, t2)
+
+        def rope_add(c, m):
+            t1, t2 = prod[(c, m)]
+            r = work.tile([P, NCH], F32, name="r%d_%d" % (c, m), tag="r", bufs=6)
+            nc.vector.tensor_tensor(
+                out=r[:].rearrange("p (j e) -> p j e", e=2),
+                in0=t1[:].rearrange("p (j e) -> p j e", e=2),
+                in1=t2[:].rearrange("p (j e) -> p j e", e=2)[:, :, ::-1],
+                op=ADD,
+            )
+            store(c, m, r[:])
+
+        def rope(c):
+            for m in range(ROW_TILES):
+                rope_mul(c, m)
+                if m > 0:
+                    rope_add(c, m - 1)
+            rope_add(c, ROW_TILES - 1)
+
+        def copy_v(m):
+            r = work.tile([P, NCH], F32, name="r5_%d" % m, tag="r", bufs=6)
+            if m % 2 == 0:
+                nc.scalar.copy(out=r[:], in_=acc[(5, m)][:])
+            else:
+                nc.vector.tensor_copy(out=r[:], in_=acc[(5, m)][:])
+            store(5, m, r[:])
+
+        for m in range(ROW_TILES):
+            transpose_x(m)
+        for i in range(ROW_TILES + 1):
+            if i < ROW_TILES:
+                widen(1, i)
+                copy_x(i)
+                interleave(0, i)
+            if i > 0:
+                quantize_w(0, i - 1)
+                quantize_x(i - 1)
+        for g in range(PASSES):
+            multiply(0, g)
+
+        for c in range(1, 5):
+            for g in range(PASSES):
+                interleave(c, g)
+            for g in range(PASSES):
+                quantize_w(c, g)
+                multiply(c, g)
+            if c < 4:
+                for g in range(PASSES):
+                    widen(c + 1, g)
+            rope(c - 1)
+
+        for g in range(PASSES):
+            interleave(5, g)
+        for m in range(ROW_TILES):
+            rope_mul(4, m)
+            if m > 0:
+                rope_add(4, m - 1)
+            quantize_w(5, m)
+            multiply(5, m)
+        rope_add(4, ROW_TILES - 1)
+        for m in range(ROW_TILES):
+            copy_v(m)

@@ -24,8 +24,10 @@ HD = 128
 
 FLOPS = 2 * TOKENS * DIM * (2048 + 512 + 512)
 
-MANUAL = False
-ON_SCALAR = {0: (), 1: (2, 3), 2: (3,), 3: (2, 3), 4: (3,), 5: (0, 1, 2, 3)}
+MANUAL = True
+ON_SCALAR = {0: (), 1: (3,), 2: (2, 3), 3: (3,), 4: (3,), 5: (0, 1, 2, 3)}
+GP_ADDS = (0, 1, 2)
+TAIL_EARLY = 3
 
 
 def tile_attention_pa_kernel(
@@ -76,18 +78,11 @@ def tile_attention_pa_kernel(
             nc.sync.dma_start(out=t[:], in_=x_rows[m * P : (m + 1) * P, :])
             x_raw[m] = t
 
-        load_wq(0, 0)
-        load_kv(0, 0)
-        load_x(0)
-        load_x(1)
-        load_kv(0, 1)
-        load_wq(0, 1)
-        load_x(2)
-        load_kv(0, 2)
-        load_x(3)
-        load_wq(0, 2)
-        load_kv(0, 3)
-        load_wq(0, 3)
+        for g in range(PASSES):
+            load_wq(0, g)
+            load_kv(0, g)
+        for m in range(ROW_TILES):
+            load_x(m)
         for j in range(1, 4):
             for g in range(PASSES):
                 load_wq(j, g)
@@ -108,8 +103,8 @@ def tile_attention_pa_kernel(
         sin2_v = sin2[:].rearrange("p m (i e) -> p (m i) e", e=2)
         nc.vector.tensor_copy(out=cos2_v[:, :, 0], in_=cos_flat)
         nc.vector.tensor_copy(out=cos2_v[:, :, 1], in_=cos_flat)
-        nc.vector.tensor_copy(out=sin2_v[:, :, 0], in_=sin_flat)
-        nc.vector.tensor_scalar_mul(out=sin2_v[:, :, 1], in0=sin_flat, scalar1=-1.0)
+        nc.vector.tensor_scalar_mul(out=sin2_v[:, :, 0], in0=sin_flat, scalar1=-1.0)
+        nc.vector.tensor_copy(out=sin2_v[:, :, 1], in_=sin_flat)
 
         x_codes = keep.tile([P, ROW_TILES, PASSES * P], U32, name="x_codes", tag="x_codes", align_bytes=64)
         x_scales = keep.tile([P, ROW_TILES, PASSES * P], U8, name="x_scales", tag="x_scales", align_bytes=64)
@@ -138,7 +133,7 @@ def tile_attention_pa_kernel(
                 x_banks[(m, h)] = bank
 
         def copy_x(m):
-            xg = work.tile([P, DIM], BF16, name="xg%d" % m, tag="xg", bufs=2, align_bytes=64)
+            xg = work.tile([P, DIM], BF16, name="xg%d" % m, tag="gr", bufs=8, align_bytes=64)
             xg_words = xg[:].bitcast(F32)
             for h in range(2):
                 nc.scalar.copy(
@@ -160,7 +155,7 @@ def tile_attention_pa_kernel(
 
         def interleave(c, g):
             src = planes[(c, g)] if 1 <= c <= 4 else wkv_raw[(c, g)]
-            gr = work.tile([P, PACK * NCH], BF16, name="gr%d_%d" % (c, g), tag="gr", bufs=6, align_bytes=64)
+            gr = work.tile([P, PACK * NCH], BF16, name="gr%d_%d" % (c, g), tag="gr", bufs=8, align_bytes=64)
             dst_v = gr[:].rearrange("p (n t) -> p n t", t=PACK)
             src_v = src[:].rearrange("p t n -> p n t")
             if g in ON_SCALAR[c]:
@@ -174,9 +169,9 @@ def tile_attention_pa_kernel(
                 out=w_codes[c][:, g, :].bitcast(FP8X4), scales=w_scales[c][:, g, :], in_=grouped[(c, g)][:]
             )
 
-        def multiply(c, g):
+        def multiply(c, g, first, last):
             for m in range(ROW_TILES):
-                if g == 0:
+                if first:
                     acc[(c, m)] = psum.tile([P, NCH], F32, name="acc%d_%d" % (c, m), tag="bank")
                 nc.tensor.matmul_mx(
                     out=acc[(c, m)][:],
@@ -184,8 +179,8 @@ def tile_attention_pa_kernel(
                     lhsT_scale=x_scales[:, m, g * P : (g + 1) * P],
                     rhs=w_codes[c][:, g, :].bitcast(FP8X4),
                     rhs_scale=w_scales[c][:, g, :],
-                    start=(g == 0),
-                    stop=(g == PASSES - 1),
+                    start=first,
+                    stop=last,
                 )
 
         def store(c, m, tile_ap):
@@ -199,20 +194,19 @@ def tile_attention_pa_kernel(
             nc.sync.dma_start(out=dst, in_=tile_ap)
 
         def rope_mul(c, m):
-            bank_v = acc[(c, m)][:].rearrange("p (h d) -> p h d", d=HD)
             t1 = work.tile([P, NCH], F32, name="t1_%d_%d" % (c, m), tag="t1", bufs=3)
             t2 = work.tile([P, NCH], F32, name="t2_%d_%d" % (c, m), tag="t2", bufs=3)
-            shape = [P, NCH // HD, HD]
+            heads = NCH // HD
             nc.vector.tensor_tensor(
                 out=t1[:].rearrange("p (h d) -> p h d", d=HD),
-                in0=bank_v,
-                in1=cos2[:, m, :].unsqueeze(1).to_broadcast(shape),
+                in0=acc[(c, m)][:].rearrange("p (h d) -> p h d", d=HD),
+                in1=cos2[:, m, :].unsqueeze(1).to_broadcast([P, heads, HD]),
                 op=MULT,
             )
             nc.vector.tensor_tensor(
-                out=t2[:].rearrange("p (h d) -> p h d", d=HD),
-                in0=bank_v,
-                in1=sin2[:, m, :].unsqueeze(1).to_broadcast(shape),
+                out=t2[:].rearrange("p (h i e) -> p h i e", h=heads, e=2),
+                in0=acc[(c, m)][:].rearrange("p (h i e) -> p h i e", h=heads, e=2)[:, :, :, ::-1],
+                in1=sin2[:, m, :].rearrange("p (i e) -> p i e", e=2).unsqueeze(1).to_broadcast([P, heads, HD // 2, 2]),
                 op=MULT,
             )
             prod[(c, m)] = (t1, t2)
@@ -220,20 +214,16 @@ def tile_attention_pa_kernel(
         def rope_add(c, m):
             t1, t2 = prod[(c, m)]
             r = work.tile([P, NCH], F32, name="r%d_%d" % (c, m), tag="r", bufs=6)
-            nc.vector.tensor_tensor(
-                out=r[:].rearrange("p (j e) -> p j e", e=2),
-                in0=t1[:].rearrange("p (j e) -> p j e", e=2),
-                in1=t2[:].rearrange("p (j e) -> p j e", e=2)[:, :, ::-1],
-                op=ADD,
-            )
+            if m in GP_ADDS:
+                nc.gpsimd.tensor_tensor(out=r[:], in0=t1[:], in1=t2[:], op=ADD)
+            else:
+                nc.vector.tensor_tensor(out=r[:], in0=t1[:], in1=t2[:], op=ADD)
             store(c, m, r[:])
 
         def rope(c):
             for m in range(ROW_TILES):
                 rope_mul(c, m)
-                if m > 0:
-                    rope_add(c, m - 1)
-            rope_add(c, ROW_TILES - 1)
+                rope_add(c, m)
 
         def copy_v(m):
             r = work.tile([P, NCH], F32, name="r5_%d" % m, tag="r", bufs=6)
@@ -243,38 +233,53 @@ def tile_attention_pa_kernel(
                 nc.vector.tensor_copy(out=r[:], in_=acc[(5, m)][:])
             store(5, m, r[:])
 
-        for m in range(ROW_TILES):
-            transpose_x(m)
-        for i in range(ROW_TILES + 1):
-            if i < ROW_TILES:
-                widen(1, i)
-                copy_x(i)
-                interleave(0, i)
-            if i > 0:
-                quantize_w(0, i - 1)
-                quantize_x(i - 1)
-        for g in range(PASSES):
-            multiply(0, g)
+        def passes_of(c):
+            on_s = [g for g in range(PASSES) if g in ON_SCALAR[c]]
+            on_v = [g for g in range(PASSES) if g not in ON_SCALAR[c]]
+            return on_v, on_s
 
-        for c in range(1, 5):
-            for g in range(PASSES):
+        def prep_scalar(c):
+            for g in passes_of(c)[1]:
                 interleave(c, g)
-            for g in range(PASSES):
-                quantize_w(c, g)
-                multiply(c, g)
             if c < 4:
                 for g in range(PASSES):
                     widen(c + 1, g)
-            rope(c - 1)
+
+        def prep_vector(c, woven):
+            on_v, on_s = passes_of(c)
+            steps = [(interleave, g) for g in on_v] + [(quantize_w, g) for g in on_v + on_s]
+            for i, (fn, g) in enumerate(steps):
+                fn(c, g)
+                if i < len(woven):
+                    quantize_x(woven[i])
+            if woven:
+                for g in range(PASSES):
+                    multiply(0, g, g == 0, g == PASSES - 1)
+            for i, g in enumerate(on_v + on_s):
+                multiply(c, g, i == 0, i == PASSES - 1)
 
         for g in range(PASSES):
-            interleave(5, g)
+            widen(1, g)
+        interleave(0, 0)
+        for g in range(1, PASSES):
+            interleave(0, g)
+            quantize_w(0, g - 1)
+        quantize_w(0, PASSES - 1)
         for m in range(ROW_TILES):
-            rope_mul(4, m)
-            if m > 0:
-                rope_add(4, m - 1)
-            quantize_w(5, m)
-            multiply(5, m)
-        rope_add(4, ROW_TILES - 1)
+            transpose_x(m)
+            copy_x(m)
+        prep_scalar(1)
+        prep_vector(1, [0, 1, 2, 3])
+        rope(0)
+        for c in range(2, 5):
+            prep_scalar(c)
+            prep_vector(c, [])
+            rope(c - 1)
+        prep_scalar(5)
+        for g in range(PASSES):
+            if g == TAIL_EARLY:
+                rope(4)
+            quantize_w(5, g)
+            multiply(5, g, g == 0, g == PASSES - 1)
         for m in range(ROW_TILES):
             copy_v(m)

@@ -25,9 +25,11 @@ HD = 128
 FLOPS = 2 * TOKENS * DIM * (2048 + 512 + 512)
 
 MANUAL = True
-ON_SCALAR = {0: (), 1: (3,), 2: (2, 3), 3: (3,), 4: (3,), 5: (0, 1, 2, 3)}
-GP_ADDS = (0, 1, 2)
+ON_SCALAR = {0: (), 1: (), 2: (), 3: (), 4: (), 5: (1, 2, 3)}
+VIA_PE = {0: (), 1: (0, 1), 2: (0, 1), 3: (0, 1), 4: (0, 1), 5: (0,)}
+GP_ADDS = (0, 1)
 TAIL_EARLY = 3
+V_COPY_ON_SCALAR = (0, 1, 2, 3)
 
 
 def tile_attention_pa_kernel(
@@ -47,7 +49,7 @@ def tile_attention_pa_kernel(
         raw = ctx.enter_context(tc.tile_pool(name="raw", bufs=1))
         keep = ctx.enter_context(tc.tile_pool(name="keep", bufs=1))
         work = ctx.enter_context(tc.tile_pool(name="work", bufs=2))
-        psum = ctx.enter_context(tc.psum_pool(name="psum", bufs=8))
+        psum = ctx.enter_context(tc.psum_pool(name="psum", bufs=4))
         if MANUAL:
             ctx.enter_context(tc.manual_schedule())
 
@@ -69,7 +71,7 @@ def tile_attention_pa_kernel(
 
         def load_kv(c, g):
             view = wk_view if c == 0 else wv_view
-            t = raw.tile([P, PACK, NCH], BF16, name="wkv%d_%d" % (c, g), tag="wkv%d_%d" % (c, g))
+            t = raw.tile([P, PACK, NCH], BF16, name="wkv%d_%d" % (c, g), tag="wkv%d" % g)
             nc.sync.dma_start(out=t[:], in_=view[g])
             wkv_raw[(c, g)] = t
 
@@ -86,25 +88,20 @@ def tile_attention_pa_kernel(
         for j in range(1, 4):
             for g in range(PASSES):
                 load_wq(j, g)
-        for g in range(PASSES):
-            load_kv(5, g)
 
         ident = const.tile([P, P], F32, name="ident", tag="ident")
         make_identity(nc, ident[:])
+        ident_bf = const.tile([P, P], BF16, name="ident_bf", tag="ident_bf")
+        make_identity(nc, ident_bf[:])
         warm = const.tile([P, 2], F32, name="warm", tag="warm")
         nc.vector.memset(warm[:, 0:1], 0.0)
         nc.scalar.activation(out=warm[:, 1:2], in_=warm[:, 0:1], func=COPY)
 
-        cos2 = const.tile([P, ROW_TILES, HD], F32, name="cos2", tag="cos2")
         sin2 = const.tile([P, ROW_TILES, HD], F32, name="sin2", tag="sin2")
-        cos_flat = cos_t[:].rearrange("p m i -> p (m i)")
         sin_flat = sin_t[:].rearrange("p m i -> p (m i)")
-        cos2_v = cos2[:].rearrange("p m (i e) -> p (m i) e", e=2)
         sin2_v = sin2[:].rearrange("p m (i e) -> p (m i) e", e=2)
-        nc.vector.tensor_copy(out=cos2_v[:, :, 0], in_=cos_flat)
-        nc.vector.tensor_copy(out=cos2_v[:, :, 1], in_=cos_flat)
-        nc.vector.tensor_scalar_mul(out=sin2_v[:, :, 0], in0=sin_flat, scalar1=-1.0)
-        nc.vector.tensor_copy(out=sin2_v[:, :, 1], in_=sin_flat)
+        nc.vector.tensor_copy(out=sin2_v[:, :, 0], in_=sin_flat)
+        nc.vector.tensor_scalar_mul(out=sin2_v[:, :, 1], in0=sin_flat, scalar1=-1.0)
 
         x_codes = keep.tile([P, ROW_TILES, PASSES * P], U32, name="x_codes", tag="x_codes", align_bytes=64)
         x_scales = keep.tile([P, ROW_TILES, PASSES * P], U8, name="x_scales", tag="x_scales", align_bytes=64)
@@ -124,7 +121,7 @@ def tile_attention_pa_kernel(
         def transpose_x(m):
             words = x_raw[m][:].bitcast(F32)
             for h in range(2):
-                bank = psum.tile([P, 512], F32, name="xt%d_%d" % (m, h), tag="bank")
+                bank = psum.tile([P, 512], F32, name="xt%d_%d" % (m, h), tag="aux", bufs=4)
                 for gl in range(2):
                     g = 2 * h + gl
                     for u in range(2):
@@ -156,31 +153,45 @@ def tile_attention_pa_kernel(
         def interleave(c, g):
             src = planes[(c, g)] if 1 <= c <= 4 else wkv_raw[(c, g)]
             gr = work.tile([P, PACK * NCH], BF16, name="gr%d_%d" % (c, g), tag="gr", bufs=8, align_bytes=64)
-            dst_v = gr[:].rearrange("p (n t) -> p n t", t=PACK)
-            src_v = src[:].rearrange("p t n -> p n t")
+            grouped[(c, g)] = gr
+            if g in VIA_PE[c]:
+                for h in range(2):
+                    bank = psum.tile([P, 1024], BF16, name="il%d_%d_%d" % (c, g, h), tag="aux", bufs=4)
+                    for q in range(2):
+                        n0 = (2 * h + q) * P
+                        nc.tensor.matmul(
+                            out=bank[:, 512 * q : 512 * (q + 1)].rearrange("p (n t) -> p n t", t=PACK),
+                            lhsT=ident_bf[:],
+                            rhs=src[:, :, n0 : n0 + P].rearrange("p t n -> p n t"),
+                            start=True,
+                            stop=True,
+                        )
+                    nc.scalar.copy(out=gr[:, 1024 * h : 1024 * (h + 1)], in_=bank[:])
+                return
+            dst_v = gr[:].rearrange("p (c i t) -> p c t i", i=4, t=PACK)
+            src_v = src[:].rearrange("p t (c i) -> p c t i", i=4)
             if g in ON_SCALAR[c]:
                 nc.scalar.copy(out=dst_v, in_=src_v)
             else:
                 nc.vector.tensor_copy(out=dst_v, in_=src_v)
-            grouped[(c, g)] = gr
 
         def quantize_w(c, g):
             nc.vector.quantize_mx(
                 out=w_codes[c][:, g, :].bitcast(FP8X4), scales=w_scales[c][:, g, :], in_=grouped[(c, g)][:]
             )
 
-        def multiply(c, g, first, last):
-            for m in range(ROW_TILES):
-                if first:
-                    acc[(c, m)] = psum.tile([P, NCH], F32, name="acc%d_%d" % (c, m), tag="bank")
+        def multiply(c, m, passes, first, last):
+            if first:
+                acc[(c, m)] = psum.tile([P, NCH], F32, name="acc%d_%d" % (c, m), tag="acc", bufs=4)
+            for i, g in enumerate(passes):
                 nc.tensor.matmul_mx(
                     out=acc[(c, m)][:],
                     lhsT=x_codes[:, m, g * P : (g + 1) * P].bitcast(FP8X4),
                     lhsT_scale=x_scales[:, m, g * P : (g + 1) * P],
                     rhs=w_codes[c][:, g, :].bitcast(FP8X4),
                     rhs_scale=w_scales[c][:, g, :],
-                    start=first,
-                    stop=last,
+                    start=(first and i == 0),
+                    stop=(last and i == len(passes) - 1),
                 )
 
         def store(c, m, tile_ap):
@@ -194,92 +205,123 @@ def tile_attention_pa_kernel(
             nc.sync.dma_start(out=dst, in_=tile_ap)
 
         def rope_mul(c, m):
-            t1 = work.tile([P, NCH], F32, name="t1_%d_%d" % (c, m), tag="t1", bufs=3)
-            t2 = work.tile([P, NCH], F32, name="t2_%d_%d" % (c, m), tag="t2", bufs=3)
+            t1 = work.tile([P, NCH], F32, name="t1_%d_%d" % (c, m), tag="t1", bufs=4)
+            t2 = work.tile([P, NCH], F32, name="t2_%d_%d" % (c, m), tag="t2", bufs=4)
             heads = NCH // HD
             nc.vector.tensor_tensor(
-                out=t1[:].rearrange("p (h d) -> p h d", d=HD),
-                in0=acc[(c, m)][:].rearrange("p (h d) -> p h d", d=HD),
-                in1=cos2[:, m, :].unsqueeze(1).to_broadcast([P, heads, HD]),
+                out=t1[:].rearrange("p (h i e) -> p h i e", h=heads, e=2),
+                in0=acc[(c, m)][:].rearrange("p (h i e) -> p h i e", h=heads, e=2),
+                in1=cos_t[:, m, :].unsqueeze(1).unsqueeze(3).to_broadcast([P, heads, HD // 2, 2]),
                 op=MULT,
             )
             nc.vector.tensor_tensor(
-                out=t2[:].rearrange("p (h i e) -> p h i e", h=heads, e=2),
-                in0=acc[(c, m)][:].rearrange("p (h i e) -> p h i e", h=heads, e=2)[:, :, :, ::-1],
-                in1=sin2[:, m, :].rearrange("p (i e) -> p i e", e=2).unsqueeze(1).to_broadcast([P, heads, HD // 2, 2]),
+                out=t2[:].rearrange("p (h d) -> p h d", d=HD),
+                in0=acc[(c, m)][:].rearrange("p (h d) -> p h d", d=HD),
+                in1=sin2[:, m, :].unsqueeze(1).to_broadcast([P, heads, HD]),
                 op=MULT,
             )
             prod[(c, m)] = (t1, t2)
 
         def rope_add(c, m):
             t1, t2 = prod[(c, m)]
-            r = work.tile([P, NCH], F32, name="r%d_%d" % (c, m), tag="r", bufs=6)
-            if m in GP_ADDS:
-                nc.gpsimd.tensor_tensor(out=r[:], in0=t1[:], in1=t2[:], op=ADD)
-            else:
-                nc.vector.tensor_tensor(out=r[:], in0=t1[:], in1=t2[:], op=ADD)
+            r = work.tile([P, NCH], F32, name="r%d_%d" % (c, m), tag="r", bufs=8)
+            eng = nc.gpsimd if m in GP_ADDS else nc.vector
+            eng.tensor_tensor(
+                out=r[:].rearrange("p (j e) -> p j e", e=2),
+                in0=t1[:].rearrange("p (j e) -> p j e", e=2),
+                in1=t2[:].rearrange("p (j e) -> p j e", e=2)[:, :, ::-1],
+                op=ADD,
+            )
             store(c, m, r[:])
 
         def rope(c):
             for m in range(ROW_TILES):
                 rope_mul(c, m)
-                rope_add(c, m)
+                if m in GP_ADDS:
+                    rope_add(c, m)
+
+        def late_adds(c):
+            for m in range(ROW_TILES):
+                if m not in GP_ADDS:
+                    rope_add(c, m)
 
         def copy_v(m):
-            r = work.tile([P, NCH], F32, name="r5_%d" % m, tag="r", bufs=6)
-            if m % 2 == 0:
+            r = work.tile([P, NCH], F32, name="r5_%d" % m, tag="r", bufs=8)
+            if m in V_COPY_ON_SCALAR:
                 nc.scalar.copy(out=r[:], in_=acc[(5, m)][:])
             else:
                 nc.vector.tensor_copy(out=r[:], in_=acc[(5, m)][:])
             store(5, m, r[:])
 
-        def passes_of(c):
-            on_s = [g for g in range(PASSES) if g in ON_SCALAR[c]]
-            on_v = [g for g in range(PASSES) if g not in ON_SCALAR[c]]
-            return on_v, on_s
+        all_passes = list(range(PASSES))
 
-        def prep_scalar(c):
-            for g in passes_of(c)[1]:
+        def on_vector(c):
+            return [g for g in all_passes if g not in ON_SCALAR[c] and g not in VIA_PE[c]]
+
+        def off_vector(c):
+            return [g for g in all_passes if g in VIA_PE[c]] + [g for g in all_passes if g in ON_SCALAR[c]]
+
+        def stage_a(c):
+            if 1 <= c <= 4:
+                for g in all_passes[:3]:
+                    widen(c, g)
+            for g in off_vector(c)[:1]:
                 interleave(c, g)
-            if c < 4:
-                for g in range(PASSES):
-                    widen(c + 1, g)
+            if 1 <= c <= 4:
+                widen(c, 3)
+
+        def stage_b(c):
+            for g in off_vector(c)[1:]:
+                interleave(c, g)
 
         def prep_vector(c, woven):
-            on_v, on_s = passes_of(c)
-            steps = [(interleave, g) for g in on_v] + [(quantize_w, g) for g in on_v + on_s]
+            steps = [(interleave, g) for g in on_vector(c)] + [(quantize_w, g) for g in off_vector(c) + on_vector(c)]
             for i, (fn, g) in enumerate(steps):
                 fn(c, g)
                 if i < len(woven):
                     quantize_x(woven[i])
-            if woven:
-                for g in range(PASSES):
-                    multiply(0, g, g == 0, g == PASSES - 1)
-            for i, g in enumerate(on_v + on_s):
-                multiply(c, g, i == 0, i == PASSES - 1)
 
-        for g in range(PASSES):
-            widen(1, g)
+        def multiply_by_pass(c, order):
+            for i, g in enumerate(order):
+                quantize_w(c, g)
+                for m in range(ROW_TILES):
+                    multiply(c, m, [g], i == 0, i == len(order) - 1)
+
+        stage_a(1)
+        stage_b(1)
         interleave(0, 0)
         for g in range(1, PASSES):
             interleave(0, g)
             quantize_w(0, g - 1)
         quantize_w(0, PASSES - 1)
+        for g in all_passes:
+            load_kv(5, g)
         for m in range(ROW_TILES):
             transpose_x(m)
             copy_x(m)
-        prep_scalar(1)
         prep_vector(1, [0, 1, 2, 3])
-        rope(0)
-        for c in range(2, 5):
-            prep_scalar(c)
-            prep_vector(c, [])
-            rope(c - 1)
-        prep_scalar(5)
-        for g in range(PASSES):
-            if g == TAIL_EARLY:
-                rope(4)
-            quantize_w(5, g)
-            multiply(5, g, g == 0, g == PASSES - 1)
         for m in range(ROW_TILES):
+            multiply(0, m, all_passes, True, True)
+        stage_a(2)
+        stage_b(2)
+        rope(0)
+        for m in range(ROW_TILES):
+            multiply(1, m, all_passes, True, True)
+        late_adds(0)
+        rope(1)
+        for c in range(2, 5):
+            stage_a(c + 1)
+            for g in on_vector(c):
+                interleave(c, g)
+            multiply_by_pass(c, off_vector(c) + on_vector(c))
+            stage_b(c + 1)
+            late_adds(c - 1)
+            if c == 4:
+                for g in off_vector(5) + on_vector(5):
+                    quantize_w(5, g)
+            rope(c)
+        for m in range(ROW_TILES):
+            multiply(5, m, all_passes, True, True)
             copy_v(m)
+            if m == 1:
+                late_adds(4)

@@ -25,11 +25,10 @@ HD = 128
 FLOPS = 2 * TOKENS * DIM * (2048 + 512 + 512)
 
 MANUAL = True
-ON_SCALAR = {0: (), 1: (), 2: (), 3: (), 4: (), 5: (1, 2, 3)}
-VIA_PE = {0: (), 1: (0, 1), 2: (0, 1), 3: (0, 1), 4: (0, 1), 5: (0,)}
-GP_ADDS = (0, 1)
+ON_SCALAR = {0: (), 1: (3,), 2: (2, 3), 3: (3,), 4: (3,), 5: (0, 1, 2, 3)}
+GP_TILES = 3
+GP_COLS = 384
 TAIL_EARLY = 3
-V_COPY_ON_SCALAR = (0, 1, 2, 3)
 
 
 def tile_attention_pa_kernel(
@@ -49,7 +48,7 @@ def tile_attention_pa_kernel(
         raw = ctx.enter_context(tc.tile_pool(name="raw", bufs=1))
         keep = ctx.enter_context(tc.tile_pool(name="keep", bufs=1))
         work = ctx.enter_context(tc.tile_pool(name="work", bufs=2))
-        psum = ctx.enter_context(tc.psum_pool(name="psum", bufs=4))
+        psum = ctx.enter_context(tc.psum_pool(name="psum", bufs=8))
         if MANUAL:
             ctx.enter_context(tc.manual_schedule())
 
@@ -91,8 +90,6 @@ def tile_attention_pa_kernel(
 
         ident = const.tile([P, P], F32, name="ident", tag="ident")
         make_identity(nc, ident[:])
-        ident_bf = const.tile([P, P], BF16, name="ident_bf", tag="ident_bf")
-        make_identity(nc, ident_bf[:])
         warm = const.tile([P, 2], F32, name="warm", tag="warm")
         nc.vector.memset(warm[:, 0:1], 0.0)
         nc.scalar.activation(out=warm[:, 1:2], in_=warm[:, 0:1], func=COPY)
@@ -100,8 +97,8 @@ def tile_attention_pa_kernel(
         sin2 = const.tile([P, ROW_TILES, HD], F32, name="sin2", tag="sin2")
         sin_flat = sin_t[:].rearrange("p m i -> p (m i)")
         sin2_v = sin2[:].rearrange("p m (i e) -> p (m i) e", e=2)
-        nc.vector.tensor_copy(out=sin2_v[:, :, 0], in_=sin_flat)
-        nc.vector.tensor_scalar_mul(out=sin2_v[:, :, 1], in0=sin_flat, scalar1=-1.0)
+        nc.vector.tensor_scalar_mul(out=sin2_v[:, :, 0], in0=sin_flat, scalar1=-1.0)
+        nc.vector.tensor_copy(out=sin2_v[:, :, 1], in_=sin_flat)
 
         x_codes = keep.tile([P, ROW_TILES, PASSES * P], U32, name="x_codes", tag="x_codes", align_bytes=64)
         x_scales = keep.tile([P, ROW_TILES, PASSES * P], U8, name="x_scales", tag="x_scales", align_bytes=64)
@@ -121,7 +118,7 @@ def tile_attention_pa_kernel(
         def transpose_x(m):
             words = x_raw[m][:].bitcast(F32)
             for h in range(2):
-                bank = psum.tile([P, 512], F32, name="xt%d_%d" % (m, h), tag="aux", bufs=4)
+                bank = psum.tile([P, 512], F32, name="xt%d_%d" % (m, h), tag="bank")
                 for gl in range(2):
                     g = 2 * h + gl
                     for u in range(2):
@@ -153,45 +150,31 @@ def tile_attention_pa_kernel(
         def interleave(c, g):
             src = planes[(c, g)] if 1 <= c <= 4 else wkv_raw[(c, g)]
             gr = work.tile([P, PACK * NCH], BF16, name="gr%d_%d" % (c, g), tag="gr", bufs=8, align_bytes=64)
-            grouped[(c, g)] = gr
-            if g in VIA_PE[c]:
-                for h in range(2):
-                    bank = psum.tile([P, 1024], BF16, name="il%d_%d_%d" % (c, g, h), tag="aux", bufs=4)
-                    for q in range(2):
-                        n0 = (2 * h + q) * P
-                        nc.tensor.matmul(
-                            out=bank[:, 512 * q : 512 * (q + 1)].rearrange("p (n t) -> p n t", t=PACK),
-                            lhsT=ident_bf[:],
-                            rhs=src[:, :, n0 : n0 + P].rearrange("p t n -> p n t"),
-                            start=True,
-                            stop=True,
-                        )
-                    nc.scalar.copy(out=gr[:, 1024 * h : 1024 * (h + 1)], in_=bank[:])
-                return
-            dst_v = gr[:].rearrange("p (c i t) -> p c t i", i=4, t=PACK)
-            src_v = src[:].rearrange("p t (c i) -> p c t i", i=4)
+            dst_v = gr[:].rearrange("p (n t) -> p n t", t=PACK)
+            src_v = src[:].rearrange("p t n -> p n t")
             if g in ON_SCALAR[c]:
                 nc.scalar.copy(out=dst_v, in_=src_v)
             else:
                 nc.vector.tensor_copy(out=dst_v, in_=src_v)
+            grouped[(c, g)] = gr
 
         def quantize_w(c, g):
             nc.vector.quantize_mx(
                 out=w_codes[c][:, g, :].bitcast(FP8X4), scales=w_scales[c][:, g, :], in_=grouped[(c, g)][:]
             )
 
-        def multiply(c, m, passes, first, last):
-            if first:
-                acc[(c, m)] = psum.tile([P, NCH], F32, name="acc%d_%d" % (c, m), tag="acc", bufs=4)
-            for i, g in enumerate(passes):
+        def multiply(c, g, first, last):
+            for m in range(ROW_TILES):
+                if first:
+                    acc[(c, m)] = psum.tile([P, NCH], F32, name="acc%d_%d" % (c, m), tag="bank")
                 nc.tensor.matmul_mx(
                     out=acc[(c, m)][:],
                     lhsT=x_codes[:, m, g * P : (g + 1) * P].bitcast(FP8X4),
                     lhsT_scale=x_scales[:, m, g * P : (g + 1) * P],
                     rhs=w_codes[c][:, g, :].bitcast(FP8X4),
                     rhs_scale=w_scales[c][:, g, :],
-                    start=(first and i == 0),
-                    stop=(last and i == len(passes) - 1),
+                    start=first,
+                    stop=last,
                 )
 
         def store(c, m, tile_ap):
@@ -204,124 +187,94 @@ def tile_attention_pa_kernel(
                 dst = q_out[rows, (c - 1) * NCH : c * NCH]
             nc.sync.dma_start(out=dst, in_=tile_ap)
 
-        def rope_mul(c, m):
-            t1 = work.tile([P, NCH], F32, name="t1_%d_%d" % (c, m), tag="t1", bufs=4)
-            t2 = work.tile([P, NCH], F32, name="t2_%d_%d" % (c, m), tag="t2", bufs=4)
-            heads = NCH // HD
-            nc.vector.tensor_tensor(
-                out=t1[:].rearrange("p (h i e) -> p h i e", h=heads, e=2),
-                in0=acc[(c, m)][:].rearrange("p (h i e) -> p h i e", h=heads, e=2),
-                in1=cos_t[:, m, :].unsqueeze(1).unsqueeze(3).to_broadcast([P, heads, HD // 2, 2]),
-                op=MULT,
-            )
-            nc.vector.tensor_tensor(
-                out=t2[:].rearrange("p (h d) -> p h d", d=HD),
-                in0=acc[(c, m)][:].rearrange("p (h d) -> p h d", d=HD),
-                in1=sin2[:, m, :].unsqueeze(1).to_broadcast([P, heads, HD]),
-                op=MULT,
-            )
-            prod[(c, m)] = (t1, t2)
-
-        def rope_add(c, m):
-            t1, t2 = prod[(c, m)]
-            r = work.tile([P, NCH], F32, name="r%d_%d" % (c, m), tag="r", bufs=8)
-            eng = nc.gpsimd if m in GP_ADDS else nc.vector
-            eng.tensor_tensor(
-                out=r[:].rearrange("p (j e) -> p j e", e=2),
-                in0=t1[:].rearrange("p (j e) -> p j e", e=2),
-                in1=t2[:].rearrange("p (j e) -> p j e", e=2)[:, :, ::-1],
-                op=ADD,
-            )
-            store(c, m, r[:])
-
         def rope(c):
+            heads = NCH // HD
+            t1 = work.tile([P, ROW_TILES, NCH], F32, name="t1_%d" % c, tag="t1", bufs=1)
+            t2 = work.tile([P, ROW_TILES, NCH], F32, name="t2_%d" % c, tag="t2", bufs=1)
+            r = work.tile([P, ROW_TILES, NCH], F32, name="r%d" % c, tag="r", bufs=2)
             for m in range(ROW_TILES):
-                rope_mul(c, m)
-                if m in GP_ADDS:
-                    rope_add(c, m)
-
-        def late_adds(c):
-            for m in range(ROW_TILES):
-                if m not in GP_ADDS:
-                    rope_add(c, m)
+                nc.vector.tensor_tensor(
+                    out=t1[:, m, :].rearrange("p (h i e) -> p h i e", h=heads, e=2),
+                    in0=acc[(c, m)][:].rearrange("p (h i e) -> p h i e", h=heads, e=2),
+                    in1=cos_t[:, m, :].unsqueeze(1).unsqueeze(3).to_broadcast([P, heads, HD // 2, 2]),
+                    op=MULT,
+                )
+                nc.vector.tensor_tensor(
+                    out=t2[:, m, :].rearrange("p (h i e) -> p h i e", h=heads, e=2),
+                    in0=acc[(c, m)][:].rearrange("p (h i e) -> p h i e", h=heads, e=2)[:, :, :, ::-1],
+                    in1=sin2[:, m, :].rearrange("p (i e) -> p i e", e=2).unsqueeze(1).to_broadcast([P, heads, HD // 2, 2]),
+                    op=MULT,
+                )
+                if m < GP_TILES:
+                    nc.gpsimd.tensor_tensor(
+                        out=r[:, m, :GP_COLS], in0=t1[:, m, :GP_COLS], in1=t2[:, m, :GP_COLS], op=ADD
+                    )
+            nc.vector.tensor_tensor(
+                out=r[:, GP_TILES:, :], in0=t1[:, GP_TILES:, :], in1=t2[:, GP_TILES:, :], op=ADD
+            )
+            if GP_COLS < NCH:
+                nc.vector.tensor_tensor(
+                    out=r[:, :GP_TILES, GP_COLS:], in0=t1[:, :GP_TILES, GP_COLS:], in1=t2[:, :GP_TILES, GP_COLS:], op=ADD
+                )
+            for m in (3, 0, 1, 2):
+                store(c, m, r[:, m, :])
 
         def copy_v(m):
-            r = work.tile([P, NCH], F32, name="r5_%d" % m, tag="r", bufs=8)
-            if m in V_COPY_ON_SCALAR:
+            r = work.tile([P, NCH], F32, name="rv%d" % m, tag="rv", bufs=4)
+            if m < 4:
                 nc.scalar.copy(out=r[:], in_=acc[(5, m)][:])
             else:
                 nc.vector.tensor_copy(out=r[:], in_=acc[(5, m)][:])
             store(5, m, r[:])
 
-        all_passes = list(range(PASSES))
+        def passes_of(c):
+            on_s = [g for g in range(PASSES) if g in ON_SCALAR[c]]
+            on_v = [g for g in range(PASSES) if g not in ON_SCALAR[c]]
+            return on_v, on_s
 
-        def on_vector(c):
-            return [g for g in all_passes if g not in ON_SCALAR[c] and g not in VIA_PE[c]]
-
-        def off_vector(c):
-            return [g for g in all_passes if g in VIA_PE[c]] + [g for g in all_passes if g in ON_SCALAR[c]]
-
-        def stage_a(c):
-            if 1 <= c <= 4:
-                for g in all_passes[:3]:
-                    widen(c, g)
-            for g in off_vector(c)[:1]:
+        def prep_scalar(c):
+            for g in passes_of(c)[1]:
                 interleave(c, g)
-            if 1 <= c <= 4:
-                widen(c, 3)
-
-        def stage_b(c):
-            for g in off_vector(c)[1:]:
-                interleave(c, g)
+            if c < 4:
+                for g in range(PASSES):
+                    widen(c + 1, g)
 
         def prep_vector(c, woven):
-            steps = [(interleave, g) for g in on_vector(c)] + [(quantize_w, g) for g in off_vector(c) + on_vector(c)]
+            on_v, on_s = passes_of(c)
+            steps = [(interleave, g) for g in on_v] + [(quantize_w, g) for g in on_v + on_s]
             for i, (fn, g) in enumerate(steps):
                 fn(c, g)
                 if i < len(woven):
                     quantize_x(woven[i])
+            if woven:
+                for g in range(PASSES):
+                    multiply(0, g, g == 0, g == PASSES - 1)
+            for i, g in enumerate(on_v + on_s):
+                multiply(c, g, i == 0, i == PASSES - 1)
 
-        def multiply_by_pass(c, order):
-            for i, g in enumerate(order):
-                quantize_w(c, g)
-                for m in range(ROW_TILES):
-                    multiply(c, m, [g], i == 0, i == len(order) - 1)
-
-        stage_a(1)
-        stage_b(1)
+        for g in range(PASSES):
+            widen(1, g)
         interleave(0, 0)
         for g in range(1, PASSES):
             interleave(0, g)
             quantize_w(0, g - 1)
         quantize_w(0, PASSES - 1)
-        for g in all_passes:
+        for g in range(PASSES):
             load_kv(5, g)
         for m in range(ROW_TILES):
             transpose_x(m)
             copy_x(m)
+        prep_scalar(1)
         prep_vector(1, [0, 1, 2, 3])
-        for m in range(ROW_TILES):
-            multiply(0, m, all_passes, True, True)
-        stage_a(2)
-        stage_b(2)
         rope(0)
-        for m in range(ROW_TILES):
-            multiply(1, m, all_passes, True, True)
-        late_adds(0)
-        rope(1)
         for c in range(2, 5):
-            stage_a(c + 1)
-            for g in on_vector(c):
-                interleave(c, g)
-            multiply_by_pass(c, off_vector(c) + on_vector(c))
-            stage_b(c + 1)
-            late_adds(c - 1)
-            if c == 4:
-                for g in off_vector(5) + on_vector(5):
-                    quantize_w(5, g)
-            rope(c)
+            prep_scalar(c)
+            prep_vector(c, [])
+            rope(c - 1)
+        prep_scalar(5)
+        for g in range(PASSES):
+            quantize_w(5, g)
+            multiply(5, g, g == 0, g == PASSES - 1)
         for m in range(ROW_TILES):
-            multiply(5, m, all_passes, True, True)
             copy_v(m)
-            if m == 1:
-                late_adds(4)
+        rope(4)

@@ -26,8 +26,7 @@ FLOPS = 2 * TOKENS * DIM * (2048 + 512 + 512)
 
 MANUAL = True
 ON_SCALAR = {0: (), 1: (3,), 2: (2, 3), 3: (3,), 4: (3,), 5: (0, 1, 2, 3)}
-GP_TILES = 3
-GP_COLS = 384
+GP_TILES = 2
 TAIL_EARLY = 3
 
 
@@ -97,8 +96,8 @@ def tile_attention_pa_kernel(
         sin2 = const.tile([P, ROW_TILES, HD], F32, name="sin2", tag="sin2")
         sin_flat = sin_t[:].rearrange("p m i -> p (m i)")
         sin2_v = sin2[:].rearrange("p m (i e) -> p (m i) e", e=2)
-        nc.vector.tensor_scalar_mul(out=sin2_v[:, :, 0], in0=sin_flat, scalar1=-1.0)
-        nc.vector.tensor_copy(out=sin2_v[:, :, 1], in_=sin_flat)
+        nc.vector.tensor_copy(out=sin2_v[:, :, 0], in_=sin_flat)
+        nc.vector.tensor_scalar_mul(out=sin2_v[:, :, 1], in0=sin_flat, scalar1=-1.0)
 
         x_codes = keep.tile([P, ROW_TILES, PASSES * P], U32, name="x_codes", tag="x_codes", align_bytes=64)
         x_scales = keep.tile([P, ROW_TILES, PASSES * P], U8, name="x_scales", tag="x_scales", align_bytes=64)
@@ -192,6 +191,17 @@ def tile_attention_pa_kernel(
             t1 = work.tile([P, ROW_TILES, NCH], F32, name="t1_%d" % c, tag="t1", bufs=1)
             t2 = work.tile([P, ROW_TILES, NCH], F32, name="t2_%d" % c, tag="t2", bufs=1)
             r = work.tile([P, ROW_TILES, NCH], F32, name="r%d" % c, tag="r", bufs=2)
+
+            def add(eng, m0, m1):
+                eng.tensor_tensor(
+                    out=r[:, m0:m1, :].rearrange("p a (j e) -> p (a j) e", e=2),
+                    in0=t1[:, m0:m1, :].rearrange("p a (j e) -> p (a j) e", e=2),
+                    in1=t2[:, m0:m1, :].rearrange("p a (j e) -> p (a j) e", e=2)[:, :, ::-1],
+                    op=ADD,
+                )
+                for m in range(m0, m1):
+                    store(c, m, r[:, m, :])
+
             for m in range(ROW_TILES):
                 nc.vector.tensor_tensor(
                     out=t1[:, m, :].rearrange("p (h i e) -> p h i e", h=heads, e=2),
@@ -200,24 +210,14 @@ def tile_attention_pa_kernel(
                     op=MULT,
                 )
                 nc.vector.tensor_tensor(
-                    out=t2[:, m, :].rearrange("p (h i e) -> p h i e", h=heads, e=2),
-                    in0=acc[(c, m)][:].rearrange("p (h i e) -> p h i e", h=heads, e=2)[:, :, :, ::-1],
-                    in1=sin2[:, m, :].rearrange("p (i e) -> p i e", e=2).unsqueeze(1).to_broadcast([P, heads, HD // 2, 2]),
+                    out=t2[:, m, :].rearrange("p (h d) -> p h d", d=HD),
+                    in0=acc[(c, m)][:].rearrange("p (h d) -> p h d", d=HD),
+                    in1=sin2[:, m, :].unsqueeze(1).to_broadcast([P, heads, HD]),
                     op=MULT,
                 )
                 if m < GP_TILES:
-                    nc.gpsimd.tensor_tensor(
-                        out=r[:, m, :GP_COLS], in0=t1[:, m, :GP_COLS], in1=t2[:, m, :GP_COLS], op=ADD
-                    )
-            nc.vector.tensor_tensor(
-                out=r[:, GP_TILES:, :], in0=t1[:, GP_TILES:, :], in1=t2[:, GP_TILES:, :], op=ADD
-            )
-            if GP_COLS < NCH:
-                nc.vector.tensor_tensor(
-                    out=r[:, :GP_TILES, GP_COLS:], in0=t1[:, :GP_TILES, GP_COLS:], in1=t2[:, :GP_TILES, GP_COLS:], op=ADD
-                )
-            for m in (3, 0, 1, 2):
-                store(c, m, r[:, m, :])
+                    add(nc.gpsimd, m, m + 1)
+            add(nc.vector, GP_TILES, ROW_TILES)
 
         def copy_v(m):
             r = work.tile([P, NCH], F32, name="rv%d" % m, tag="rv", bufs=4)

@@ -21,13 +21,14 @@ PASSES = 4
 NCH = 512
 ROW_TILES = 4
 HD = 128
+CHUNKS = 6
 
 FLOPS = 2 * TOKENS * DIM * (2048 + 512 + 512)
 
-MANUAL = True
-ON_SCALAR = {0: (), 1: (3,), 2: (2, 3), 3: (3,), 4: (3,), 5: (0, 1, 2, 3)}
+ON_TENSOR = {0: (), 1: (3,), 2: (2, 3), 3: (2, 3), 4: (2, 3), 5: (2, 3)}
+ON_SCALAR = {0: (), 1: (), 2: (), 3: (), 4: (), 5: (0, 1)}
 GP_TILES = 2
-TAIL_EARLY = 3
+T_FIRST = False
 
 
 def tile_attention_pa_kernel(
@@ -46,10 +47,9 @@ def tile_attention_pa_kernel(
         const = ctx.enter_context(tc.tile_pool(name="const", bufs=1))
         raw = ctx.enter_context(tc.tile_pool(name="raw", bufs=1))
         keep = ctx.enter_context(tc.tile_pool(name="keep", bufs=1))
-        work = ctx.enter_context(tc.tile_pool(name="work", bufs=2))
-        psum = ctx.enter_context(tc.psum_pool(name="psum", bufs=8))
-        if MANUAL:
-            ctx.enter_context(tc.manual_schedule())
+        work = ctx.enter_context(tc.tile_pool(name="work", bufs=1))
+        psum = ctx.enter_context(tc.psum_pool(name="psum", bufs=1))
+        ctx.enter_context(tc.manual_schedule())
 
         wsc = const.tile([P, PASSES, PACK], F32, name="wsc", tag="wsc")
         nc.scalar.dma_start(out=wsc[:], in_=wq_scale.rearrange("(g p t) o -> p g (t o)", p=P, t=PACK))
@@ -62,62 +62,77 @@ def tile_attention_pa_kernel(
         wkv_raw = {}
         x_raw = {}
 
-        def load_wq(j, g):
-            t = raw.tile([P, PACK, NCH], U8, name="wqb%d_%d" % (j, g), tag="wqb%d_%d" % (j, g))
-            nc.sync.dma_start(out=t[:], in_=wq_view[g, :, :, j * NCH : (j + 1) * NCH])
-            wq_b[(j + 1, g)] = t
+        def load_wq(c, g):
+            t = raw.tile([P, PACK, NCH], U8, name="wqb%d_%d" % (c, g), tag="wqb%d_%d" % (c, g))
+            nc.sync.dma_start(out=t[:], in_=wq_view[g, :, :, (c - 1) * NCH : c * NCH])
+            wq_b[(c, g)] = t
 
         def load_kv(c, g):
             view = wk_view if c == 0 else wv_view
-            t = raw.tile([P, PACK, NCH], BF16, name="wkv%d_%d" % (c, g), tag="wkv%d" % g)
+            t = raw.tile([P, PACK, NCH], BF16, name="wkv%d_%d" % (c, g), tag="wkv%d_%d" % (c, g))
             nc.sync.dma_start(out=t[:], in_=view[g])
             wkv_raw[(c, g)] = t
 
         def load_x(m):
-            t = work.tile([P, DIM], BF16, name="xraw%d" % m, tag="plane", bufs=8)
+            t = work.tile([P, DIM], BF16, name="xraw%d" % m, tag="pl%d" % (4 + m))
             nc.sync.dma_start(out=t[:], in_=x_rows[m * P : (m + 1) * P, :])
             x_raw[m] = t
 
         for g in range(PASSES):
-            load_wq(0, g)
+            load_wq(1, g)
             load_kv(0, g)
         for m in range(ROW_TILES):
             load_x(m)
-        for j in range(1, 4):
-            for g in range(PASSES):
-                load_wq(j, g)
+        for g in range(PASSES):
+            load_wq(2, g)
+        for g in range(PASSES):
+            load_wq(3, g)
+        for g in range(PASSES):
+            load_kv(5, g)
+        for g in range(PASSES):
+            load_wq(4, g)
 
         ident = const.tile([P, P], F32, name="ident", tag="ident")
         make_identity(nc, ident[:])
+        ident_bf = const.tile([P, P], BF16, name="ident_bf", tag="ident_bf")
+        make_identity(nc, ident_bf[:])
         warm = const.tile([P, 2], F32, name="warm", tag="warm")
         nc.vector.memset(warm[:, 0:1], 0.0)
         nc.scalar.activation(out=warm[:, 1:2], in_=warm[:, 0:1], func=COPY)
-
         sin2 = const.tile([P, ROW_TILES, HD], F32, name="sin2", tag="sin2")
-        sin_flat = sin_t[:].rearrange("p m i -> p (m i)")
-        sin2_v = sin2[:].rearrange("p m (i e) -> p (m i) e", e=2)
-        nc.vector.tensor_copy(out=sin2_v[:, :, 0], in_=sin_flat)
-        nc.vector.tensor_scalar_mul(out=sin2_v[:, :, 1], in0=sin_flat, scalar1=-1.0)
 
         x_codes = keep.tile([P, ROW_TILES, PASSES * P], U32, name="x_codes", tag="x_codes", align_bytes=64)
         x_scales = keep.tile([P, ROW_TILES, PASSES * P], U8, name="x_scales", tag="x_scales", align_bytes=64)
         w_codes = {}
         w_scales = {}
-        for c in range(6):
-            w_codes[c] = keep.tile([P, PASSES, NCH], U32, name="w_codes%d" % c, tag="w_codes%d" % c, align_bytes=64)
-            w_scales[c] = keep.tile([P, PASSES, NCH], U8, name="w_scales%d" % c, tag="w_scales%d" % c, align_bytes=64)
-
         planes = {}
         grouped = {}
         x_banks = {}
         x_grouped = {}
+        il_banks = {}
         acc = {}
-        prod = {}
+        rot = {}
+
+        tensor_passes = [(c, g) for c in range(CHUNKS) for g in ON_TENSOR[c]]
+
+        def maker(c, g):
+            if g in ON_TENSOR[c]:
+                return ("IL", c, g)
+            return ("IS", c, g) if g in ON_SCALAR[c] else ("IV", c, g)
+
+        def grouper(c, g):
+            return ("E", c, g) if g in ON_TENSOR[c] else maker(c, g)
+
+        def sin_table():
+            sin_flat = sin_t[:].rearrange("p m i -> p (m i)")
+            sin2_v = sin2[:].rearrange("p m (i e) -> p (m i) e", e=2)
+            nc.vector.tensor_copy(out=sin2_v[:, :, 0], in_=sin_flat)
+            nc.vector.tensor_scalar_mul(out=sin2_v[:, :, 1], in0=sin_flat, scalar1=-1.0)
 
         def transpose_x(m):
             words = x_raw[m][:].bitcast(F32)
             for h in range(2):
-                bank = psum.tile([P, 512], F32, name="xt%d_%d" % (m, h), tag="bank")
+                bank = psum.tile([P, 512], F32, name="xt%d_%d" % (m, h), tag="b%d" % (2 * m + h))
                 for gl in range(2):
                     g = 2 * h + gl
                     for u in range(2):
@@ -126,7 +141,7 @@ def tile_attention_pa_kernel(
                 x_banks[(m, h)] = bank
 
         def copy_x(m):
-            xg = work.tile([P, DIM], BF16, name="xg%d" % m, tag="gr", bufs=8, align_bytes=64)
+            xg = work.tile([P, DIM], BF16, name="xg%d" % m, tag="xg%d" % m, align_bytes=64)
             xg_words = xg[:].bitcast(F32)
             for h in range(2):
                 nc.scalar.copy(
@@ -139,44 +154,83 @@ def tile_attention_pa_kernel(
             nc.vector.quantize_mx(out=x_codes[:, m, :].bitcast(FP8X4), scales=x_scales[:, m, :], in_=x_grouped[m][:])
 
         def widen(c, g):
-            pl = work.tile([P, PACK, NCH], BF16, name="pl%d_%d" % (c, g), tag="plane", bufs=8)
+            pl = work.tile([P, PACK, NCH], BF16, name="pl%d_%d" % (c, g), tag="pl%d" % ((4 * (c - 1) + g) % 8))
             for t in range(PACK):
                 nc.scalar.activation(
                     out=pl[:, t, :], in_=wq_b[(c, g)][:, t, :].bitcast(FP8), func=COPY, scale=wsc[:, g, t : t + 1]
                 )
             planes[(c, g)] = pl
 
-        def interleave(c, g):
-            src = planes[(c, g)] if 1 <= c <= 4 else wkv_raw[(c, g)]
-            gr = work.tile([P, PACK * NCH], BF16, name="gr%d_%d" % (c, g), tag="gr", bufs=8, align_bytes=64)
-            dst_v = gr[:].rearrange("p (n t) -> p n t", t=PACK)
-            src_v = src[:].rearrange("p t n -> p n t")
-            if g in ON_SCALAR[c]:
-                nc.scalar.copy(out=dst_v, in_=src_v)
-            else:
-                nc.vector.tensor_copy(out=dst_v, in_=src_v)
+        def source(c, g):
+            return planes[(c, g)] if 1 <= c <= 4 else wkv_raw[(c, g)]
+
+        def new_grouped(c, g):
+            gr = work.tile(
+                [P, PACK * NCH], BF16, name="gr%d_%d" % (c, g), tag="gr%d" % ((4 * c + g) % 8), align_bytes=64
+            )
             grouped[(c, g)] = gr
+            return gr
+
+        def interleave(eng_copy, c, g):
+            gr = new_grouped(c, g)
+            eng_copy(out=gr[:].rearrange("p (n t) -> p n t", t=PACK), in_=source(c, g)[:].rearrange("p t n -> p n t"))
+
+        def tensor_interleave(c, g):
+            pair = tensor_passes.index((c, g)) % 2
+            src = source(c, g)
+            for h in range(2):
+                bank = psum.tile([P, 2 * NCH], BF16, name="il%d_%d_%d" % (c, g, h), tag="b%d" % (4 + 2 * pair + h))
+                for q in range(2):
+                    n0 = (2 * h + q) * P
+                    nc.tensor.matmul(
+                        out=bank[:, q * NCH : (q + 1) * NCH],
+                        lhsT=ident_bf[:],
+                        rhs=src[:, :, n0 : n0 + P].rearrange("p t n -> p n t"),
+                        start=True,
+                        stop=True,
+                    )
+                il_banks[(c, g, h)] = bank
+
+        def evacuate(c, g):
+            words = new_grouped(c, g)[:].bitcast(F32)
+            for h in range(2):
+                nc.scalar.copy(out=words[:, h * NCH : (h + 1) * NCH], in_=il_banks[(c, g, h)][:].bitcast(F32))
 
         def quantize_w(c, g):
+            if g == first_quantized[c]:
+                w_codes[c] = keep.tile(
+                    [P, PASSES, NCH], U32, name="w_codes%d" % c, tag="w_codes%d" % (c % 3), align_bytes=64
+                )
+                w_scales[c] = keep.tile(
+                    [P, PASSES, NCH], U8, name="w_scales%d" % c, tag="w_scales%d" % (c % 3), align_bytes=64
+                )
             nc.vector.quantize_mx(
                 out=w_codes[c][:, g, :].bitcast(FP8X4), scales=w_scales[c][:, g, :], in_=grouped[(c, g)][:]
             )
 
-        def multiply(c, g, first, last):
-            for m in range(ROW_TILES):
-                if first:
-                    acc[(c, m)] = psum.tile([P, NCH], F32, name="acc%d_%d" % (c, m), tag="bank")
-                nc.tensor.matmul_mx(
-                    out=acc[(c, m)][:],
-                    lhsT=x_codes[:, m, g * P : (g + 1) * P].bitcast(FP8X4),
-                    lhsT_scale=x_scales[:, m, g * P : (g + 1) * P],
-                    rhs=w_codes[c][:, g, :].bitcast(FP8X4),
-                    rhs_scale=w_scales[c][:, g, :],
-                    start=first,
-                    stop=last,
-                )
+        def one_matmul(c, m, g, first, last):
+            if first:
+                acc[(c, m)] = psum.tile([P, NCH], F32, name="acc%d_%d" % (c, m), tag="b%d" % (m if c < 5 else 4 + m))
+            nc.tensor.matmul_mx(
+                out=acc[(c, m)][:],
+                lhsT=x_codes[:, m, g * P : (g + 1) * P].bitcast(FP8X4),
+                lhsT_scale=x_scales[:, m, g * P : (g + 1) * P],
+                rhs=w_codes[c][:, g, :].bitcast(FP8X4),
+                rhs_scale=w_scales[c][:, g, :],
+                start=first,
+                stop=last,
+            )
 
-        def store(c, m, tile_ap):
+        def multiply_tile(c, m):
+            for g in range(PASSES):
+                one_matmul(c, m, g, g == 0, g == PASSES - 1)
+
+        def multiply_pass(c, i):
+            g = quant_order[c][i]
+            for m in range(ROW_TILES):
+                one_matmul(c, m, g, i == 0, i == PASSES - 1)
+
+        def store(c, m, tile_ap, queue=None):
             rows = slice(m * P, (m + 1) * P)
             if c == 0:
                 dst = k_out[rows, :]
@@ -184,97 +238,186 @@ def tile_attention_pa_kernel(
                 dst = v_out[rows, :]
             else:
                 dst = q_out[rows, (c - 1) * NCH : c * NCH]
-            nc.sync.dma_start(out=dst, in_=tile_ap)
+            (queue or nc.sync).dma_start(out=dst, in_=tile_ap)
 
-        def rope(c):
+        def add(eng, c, m0, m1):
+            t1, t2, r = rot[c]
+            eng.tensor_tensor(
+                out=r[:, m0:m1, :].rearrange("p a (j e) -> p (a j) e", e=2),
+                in0=t1[:, m0:m1, :].rearrange("p a (j e) -> p (a j) e", e=2),
+                in1=t2[:, m0:m1, :].rearrange("p a (j e) -> p (a j) e", e=2)[:, :, ::-1],
+                op=ADD,
+            )
+            for m in range(m0, m1):
+                store(c, m, r[:, m, :])
+
+        def products(c, m):
             heads = NCH // HD
-            t1 = work.tile([P, ROW_TILES, NCH], F32, name="t1_%d" % c, tag="t1", bufs=1)
-            t2 = work.tile([P, ROW_TILES, NCH], F32, name="t2_%d" % c, tag="t2", bufs=1)
-            r = work.tile([P, ROW_TILES, NCH], F32, name="r%d" % c, tag="r", bufs=2)
-
-            def add(eng, m0, m1):
-                eng.tensor_tensor(
-                    out=r[:, m0:m1, :].rearrange("p a (j e) -> p (a j) e", e=2),
-                    in0=t1[:, m0:m1, :].rearrange("p a (j e) -> p (a j) e", e=2),
-                    in1=t2[:, m0:m1, :].rearrange("p a (j e) -> p (a j) e", e=2)[:, :, ::-1],
-                    op=ADD,
+            if m == 0:
+                rot[c] = (
+                    work.tile([P, ROW_TILES, NCH], F32, name="t1_%d" % c, tag="t1"),
+                    work.tile([P, ROW_TILES, NCH], F32, name="t2_%d" % c, tag="t2"),
+                    work.tile([P, ROW_TILES, NCH], F32, name="r%d" % c, tag="r%d" % (c % 2)),
                 )
-                for m in range(m0, m1):
-                    store(c, m, r[:, m, :])
-
-            for m in range(ROW_TILES):
-                nc.vector.tensor_tensor(
-                    out=t1[:, m, :].rearrange("p (h i e) -> p h i e", h=heads, e=2),
-                    in0=acc[(c, m)][:].rearrange("p (h i e) -> p h i e", h=heads, e=2),
-                    in1=cos_t[:, m, :].unsqueeze(1).unsqueeze(3).to_broadcast([P, heads, HD // 2, 2]),
-                    op=MULT,
-                )
-                nc.vector.tensor_tensor(
-                    out=t2[:, m, :].rearrange("p (h d) -> p h d", d=HD),
-                    in0=acc[(c, m)][:].rearrange("p (h d) -> p h d", d=HD),
-                    in1=sin2[:, m, :].unsqueeze(1).to_broadcast([P, heads, HD]),
-                    op=MULT,
-                )
-                if m < GP_TILES:
-                    add(nc.gpsimd, m, m + 1)
-            add(nc.vector, GP_TILES, ROW_TILES)
+            t1, t2, r = rot[c]
+            nc.vector.tensor_tensor(
+                out=t1[:, m, :].rearrange("p (h i e) -> p h i e", h=heads, e=2),
+                in0=acc[(c, m)][:].rearrange("p (h i e) -> p h i e", h=heads, e=2),
+                in1=cos_t[:, m, :].unsqueeze(1).unsqueeze(3).to_broadcast([P, heads, HD // 2, 2]),
+                op=MULT,
+            )
+            nc.vector.tensor_tensor(
+                out=t2[:, m, :].rearrange("p (h d) -> p h d", d=HD),
+                in0=acc[(c, m)][:].rearrange("p (h d) -> p h d", d=HD),
+                in1=sin2[:, m, :].unsqueeze(1).to_broadcast([P, heads, HD]),
+                op=MULT,
+            )
+            if m < GP_TILES:
+                add(nc.gpsimd, c, m, m + 1)
 
         def copy_v(m):
-            r = work.tile([P, NCH], F32, name="rv%d" % m, tag="rv", bufs=4)
-            if m < 4:
-                nc.scalar.copy(out=r[:], in_=acc[(5, m)][:])
+            r = work.tile([P, NCH], F32, name="rv%d" % m, tag="rv%d" % m)
+            nc.scalar.copy(out=r[:], in_=acc[(5, m)][:])
+            store(5, m, r[:], nc.scalar)
+
+        on_vector = {c: tuple(g for g in range(PASSES) if g not in ON_TENSOR[c] + ON_SCALAR[c]) for c in range(CHUNKS)}
+        others = {c: ON_SCALAR[c] + ON_TENSOR[c] for c in range(CHUNKS)}
+        quant_order = {c: (others[c] + on_vector[c]) if T_FIRST else (on_vector[c] + others[c]) for c in range(CHUNKS)}
+        widen_order = {c: (ON_TENSOR[c] + on_vector[c] + ON_SCALAR[c]) if T_FIRST else (on_vector[c] + others[c]) for c in range(CHUNKS)}
+        first_quantized = {c: quant_order[c][0] for c in range(CHUNKS)}
+
+        def vector_prep(c):
+            seq = []
+            if T_FIRST:
+                for j, g in enumerate(on_vector[c]):
+                    seq.append(("IV", c, g))
+                    if j < len(others[c]):
+                        seq.append(("Q", c, others[c][j]))
+                seq += [("Q", c, g) for g in others[c][len(on_vector[c]) :]]
+                seq += [("Q", c, g) for g in on_vector[c]]
             else:
-                nc.vector.tensor_copy(out=r[:], in_=acc[(5, m)][:])
-            store(5, m, r[:])
+                for j, g in enumerate(on_vector[c]):
+                    seq.append(("IV", c, g))
+                    if j >= 1:
+                        seq.append(("Q", c, on_vector[c][j - 1]))
+                seq += [("Q", c, g) for g in on_vector[c][-1:]]
+                seq += [("Q", c, g) for g in others[c]]
+            return seq
 
-        def passes_of(c):
-            on_s = [g for g in range(PASSES) if g in ON_SCALAR[c]]
-            on_v = [g for g in range(PASSES) if g not in ON_SCALAR[c]]
-            return on_v, on_s
+        def rope(c):
+            return [("RP", c, m) for m in range(ROW_TILES)] + [("RA", c, 0)]
 
-        def prep_scalar(c):
-            for g in passes_of(c)[1]:
-                interleave(c, g)
-            if c < 4:
-                for g in range(PASSES):
-                    widen(c + 1, g)
+        v_list = vector_prep(0) + [("SIN", 0, 0)]
+        prep1 = vector_prep(1)
+        for i, step in enumerate(prep1):
+            v_list.append(step)
+            if i < ROW_TILES:
+                v_list.append(("QX", 0, i))
+        for c in range(2, CHUNKS):
+            v_list += rope(c - 2) + vector_prep(c)
+        v_list += rope(4)
 
-        def prep_vector(c, woven):
-            on_v, on_s = passes_of(c)
-            steps = [(interleave, g) for g in on_v] + [(quantize_w, g) for g in on_v + on_s]
-            for i, (fn, g) in enumerate(steps):
-                fn(c, g)
-                if i < len(woven):
-                    quantize_x(woven[i])
-            if woven:
-                for g in range(PASSES):
-                    multiply(0, g, g == 0, g == PASSES - 1)
-            for i, g in enumerate(on_v + on_s):
-                multiply(c, g, i == 0, i == PASSES - 1)
+        s_list = []
+        waiting = []
+        for c in range(1, 5):
+            for g in widen_order[c]:
+                s_list.append(("W", c, g))
+                s_list += waiting
+                waiting = [("E", c, g)] if g in ON_TENSOR[c] else []
+                if g in ON_SCALAR[c]:
+                    s_list.append(("IS", c, g))
+            if c == 1:
+                s_list += [("XE", 0, m) for m in range(ROW_TILES)]
+        for g in ON_SCALAR[5]:
+            s_list.append(("IS", 5, g))
+            s_list += waiting
+            waiting = []
+        s_list += waiting + [("E", 5, g) for g in ON_TENSOR[5]] + [("VE", 5, m) for m in range(ROW_TILES)]
 
-        for g in range(PASSES):
-            widen(1, g)
-        interleave(0, 0)
-        for g in range(1, PASSES):
-            interleave(0, g)
-            quantize_w(0, g - 1)
-        quantize_w(0, PASSES - 1)
-        for g in range(PASSES):
-            load_kv(5, g)
-        for m in range(ROW_TILES):
-            transpose_x(m)
-            copy_x(m)
-        prep_scalar(1)
-        prep_vector(1, [0, 1, 2, 3])
-        rope(0)
-        for c in range(2, 5):
-            prep_scalar(c)
-            prep_vector(c, [])
-            rope(c - 1)
-        prep_scalar(5)
-        for g in range(PASSES):
-            quantize_w(5, g)
-            multiply(5, g, g == 0, g == PASSES - 1)
-        for m in range(ROW_TILES):
-            copy_v(m)
-        rope(4)
+        t_list = [("TX", 0, m) for m in range(ROW_TILES)] + [("IL", 1, g) for g in ON_TENSOR[1]]
+        t_list += [("MT", 0, m) for m in range(ROW_TILES)]
+        for c in range(1, 5):
+            t_list += [("IL", c + 1, g) for g in ON_TENSOR[c + 1]] + [("MT", c, m) for m in range(ROW_TILES)]
+        t_list += [("MP", 5, i) for i in range(PASSES)]
+
+        def needs(step):
+            kind, c, g = step
+            out = []
+            if kind == "W":
+                out += [("TX", 0, g)] if c == 2 else ([maker(c - 2, g)] if c > 2 else [])
+            if kind in ("IV", "IS", "IL") and 1 <= c <= 4:
+                out.append(("W", c, g))
+            if kind in ("IV", "IS", "E") and c >= 2:
+                out.append(("Q", c - 2, g))
+            if kind == "IL":
+                k = tensor_passes.index((c, g))
+                out.append(("XE", 0, 2 + k) if k < 2 else ("E",) + tensor_passes[k - 2])
+            if kind == "E":
+                out.append(("IL", c, g))
+            if kind == "Q":
+                out.append(grouper(c, g))
+                if c >= 3:
+                    out.append(("MT", c - 3, ROW_TILES - 1))
+            if kind == "XE":
+                out.append(("TX", 0, g))
+            if kind == "QX":
+                out.append(("XE", 0, g))
+            if kind == "MT":
+                out += [("Q", c, j) for j in range(PASSES)] + [("QX", 0, g)]
+                out.append(("XE", 0, g // 2) if c == 0 else ("RP", c - 1, g))
+            if kind == "MP":
+                out += [("Q", c, quant_order[c][g])] + [("QX", 0, m) for m in range(ROW_TILES)]
+                out += [("E",) + p for p in tensor_passes[-2:]]
+            if kind == "RP":
+                out += [("MT", c, g), ("SIN", 0, 0)]
+            if kind == "RA":
+                out.append(("RP", c, ROW_TILES - 1))
+            if kind == "VE":
+                out.append(("MP", 5, PASSES - 1))
+            return out
+
+        def emit(step):
+            kind, c, g = step
+            if kind == "W":
+                widen(c, g)
+            elif kind == "IV":
+                interleave(nc.vector.tensor_copy, c, g)
+            elif kind == "IS":
+                interleave(nc.scalar.copy, c, g)
+            elif kind == "IL":
+                tensor_interleave(c, g)
+            elif kind == "E":
+                evacuate(c, g)
+            elif kind == "Q":
+                quantize_w(c, g)
+            elif kind == "TX":
+                transpose_x(g)
+            elif kind == "XE":
+                copy_x(g)
+            elif kind == "QX":
+                quantize_x(g)
+            elif kind == "MT":
+                multiply_tile(c, g)
+            elif kind == "MP":
+                multiply_pass(c, g)
+            elif kind == "RP":
+                products(c, g)
+            elif kind == "RA":
+                add(nc.vector, c, GP_TILES, ROW_TILES)
+            elif kind == "VE":
+                copy_v(g)
+            else:
+                sin_table()
+
+        lists = [s_list, v_list, t_list]
+        at = [0, 0, 0]
+        done = set()
+        while any(at[i] < len(lists[i]) for i in range(3)):
+            moved = False
+            for i in range(3):
+                while at[i] < len(lists[i]) and all(n in done for n in needs(lists[i][at[i]])):
+                    emit(lists[i][at[i]])
+                    done.add(lists[i][at[i]])
+                    at[i] += 1
+                    moved = True
+            assert moved, "the three orders wait for each other"

@@ -29,6 +29,7 @@ ON_TENSOR = {0: (), 1: (3,), 2: (2, 3), 3: (2, 3), 4: (2, 3), 5: (2, 3)}
 ON_SCALAR = {0: (), 1: (), 2: (), 3: (), 4: (), 5: (0, 1)}
 GP_TILES = 2
 T_FIRST = False
+E_LATE = False
 
 
 def tile_attention_pa_kernel(
@@ -78,9 +79,9 @@ def tile_attention_pa_kernel(
             nc.sync.dma_start(out=t[:], in_=x_rows[m * P : (m + 1) * P, :])
             x_raw[m] = t
 
-        for g in range(PASSES):
+        for i, g in enumerate(ON_TENSOR[1] + tuple(j for j in range(PASSES) if j not in ON_TENSOR[1])):
             load_wq(1, g)
-            load_kv(0, g)
+            load_kv(0, i)
         for m in range(ROW_TILES):
             load_x(m)
         for g in range(PASSES):
@@ -99,7 +100,7 @@ def tile_attention_pa_kernel(
         warm = const.tile([P, 2], F32, name="warm", tag="warm")
         nc.vector.memset(warm[:, 0:1], 0.0)
         nc.scalar.activation(out=warm[:, 1:2], in_=warm[:, 0:1], func=COPY)
-        sin2 = const.tile([P, ROW_TILES, HD], F32, name="sin2", tag="sin2")
+        table = const.tile([P, ROW_TILES, 2, HD], F32, name="table", tag="table")
 
         x_codes = keep.tile([P, ROW_TILES, PASSES * P], U32, name="x_codes", tag="x_codes", align_bytes=64)
         x_scales = keep.tile([P, ROW_TILES, PASSES * P], U8, name="x_scales", tag="x_scales", align_bytes=64)
@@ -124,10 +125,11 @@ def tile_attention_pa_kernel(
             return ("E", c, g) if g in ON_TENSOR[c] else maker(c, g)
 
         def sin_table():
-            sin_flat = sin_t[:].rearrange("p m i -> p (m i)")
-            sin2_v = sin2[:].rearrange("p m (i e) -> p (m i) e", e=2)
-            nc.vector.tensor_copy(out=sin2_v[:, :, 0], in_=sin_flat)
-            nc.vector.tensor_scalar_mul(out=sin2_v[:, :, 1], in0=sin_flat, scalar1=-1.0)
+            pairs = table[:].rearrange("p m a (i e) -> p m a i e", e=2)
+            for e in range(2):
+                nc.vector.tensor_copy(out=pairs[:, :, 0, :, e], in_=cos_t[:])
+            nc.vector.tensor_copy(out=pairs[:, :, 1, :, 0], in_=sin_t[:])
+            nc.vector.tensor_scalar_mul(out=pairs[:, :, 1, :, 1], in0=sin_t[:], scalar1=-1.0)
 
         def transpose_x(m):
             words = x_raw[m][:].bitcast(F32)
@@ -173,7 +175,10 @@ def tile_attention_pa_kernel(
 
         def interleave(eng_copy, c, g):
             gr = new_grouped(c, g)
-            eng_copy(out=gr[:].rearrange("p (n t) -> p n t", t=PACK), in_=source(c, g)[:].rearrange("p t n -> p n t"))
+            eng_copy(
+                out=gr[:].rearrange("p (c i t) -> p c t i", i=4, t=PACK),
+                in_=source(c, g)[:].rearrange("p t (c i) -> p c t i", i=4),
+            )
 
         def tensor_interleave(c, g):
             pair = tensor_passes.index((c, g)) % 2
@@ -241,11 +246,11 @@ def tile_attention_pa_kernel(
             (queue or nc.sync).dma_start(out=dst, in_=tile_ap)
 
         def add(eng, c, m0, m1):
-            t1, t2, r = rot[c]
+            both, r = rot[c]
             eng.tensor_tensor(
-                out=r[:, m0:m1, :].rearrange("p a (j e) -> p (a j) e", e=2),
-                in0=t1[:, m0:m1, :].rearrange("p a (j e) -> p (a j) e", e=2),
-                in1=t2[:, m0:m1, :].rearrange("p a (j e) -> p (a j) e", e=2)[:, :, ::-1],
+                out=r[:, m0:m1, :].rearrange("p a (j e) -> p a j e", e=2),
+                in0=both[:, m0:m1, 0, :].rearrange("p a (j e) -> p a j e", e=2),
+                in1=both[:, m0:m1, 1, :].rearrange("p a (j e) -> p a j e", e=2)[:, :, :, ::-1],
                 op=ADD,
             )
             for m in range(m0, m1):
@@ -255,21 +260,14 @@ def tile_attention_pa_kernel(
             heads = NCH // HD
             if m == 0:
                 rot[c] = (
-                    work.tile([P, ROW_TILES, NCH], F32, name="t1_%d" % c, tag="t1"),
-                    work.tile([P, ROW_TILES, NCH], F32, name="t2_%d" % c, tag="t2"),
+                    work.tile([P, ROW_TILES, 2, NCH], F32, name="both%d" % c, tag="both"),
                     work.tile([P, ROW_TILES, NCH], F32, name="r%d" % c, tag="r%d" % (c % 2)),
                 )
-            t1, t2, r = rot[c]
+            both, r = rot[c]
             nc.vector.tensor_tensor(
-                out=t1[:, m, :].rearrange("p (h i e) -> p h i e", h=heads, e=2),
-                in0=acc[(c, m)][:].rearrange("p (h i e) -> p h i e", h=heads, e=2),
-                in1=cos_t[:, m, :].unsqueeze(1).unsqueeze(3).to_broadcast([P, heads, HD // 2, 2]),
-                op=MULT,
-            )
-            nc.vector.tensor_tensor(
-                out=t2[:, m, :].rearrange("p (h d) -> p h d", d=HD),
-                in0=acc[(c, m)][:].rearrange("p (h d) -> p h d", d=HD),
-                in1=sin2[:, m, :].unsqueeze(1).to_broadcast([P, heads, HD]),
+                out=both[:, m, :, :].rearrange("p a (h d) -> p a h d", d=HD),
+                in0=acc[(c, m)][:].rearrange("p (h d) -> p h d", d=HD).unsqueeze(1).to_broadcast([P, 2, heads, HD]),
+                in1=table[:, m, :, :].unsqueeze(2).to_broadcast([P, 2, heads, HD]),
                 op=MULT,
             )
             if m < GP_TILES:
@@ -316,22 +314,31 @@ def tile_attention_pa_kernel(
         for c in range(2, CHUNKS):
             v_list += rope(c - 2) + vector_prep(c)
         v_list += rope(4)
+        for i in range(len(v_list) - 1):
+            if v_list[i][0] == "RA" and v_list[i - 1][0] == "RP":
+                v_list[i], v_list[i + 1] = v_list[i + 1], v_list[i]
 
         s_list = []
         waiting = []
         for c in range(1, 5):
-            for g in widen_order[c]:
+            for g in ON_TENSOR[c] + on_vector[c] + ON_SCALAR[c]:
                 s_list.append(("W", c, g))
-                s_list += waiting
-                waiting = [("E", c, g)] if g in ON_TENSOR[c] else []
+                if E_LATE and c > 1:
+                    s_list += waiting[:1]
+                    waiting = waiting[1:]
                 if g in ON_SCALAR[c]:
                     s_list.append(("IS", c, g))
             if c == 1:
                 s_list += [("XE", 0, m) for m in range(ROW_TILES)]
+            s_list += waiting
+            waiting = [("E", c, g) for g in ON_TENSOR[c]]
+            if not E_LATE:
+                s_list += waiting
+                waiting = []
         for g in ON_SCALAR[5]:
             s_list.append(("IS", 5, g))
-            s_list += waiting
-            waiting = []
+            s_list += waiting[:1]
+            waiting = waiting[1:]
         s_list += waiting + [("E", 5, g) for g in ON_TENSOR[5]] + [("VE", 5, m) for m in range(ROW_TILES)]
 
         t_list = [("TX", 0, m) for m in range(ROW_TILES)] + [("IL", 1, g) for g in ON_TENSOR[1]]

@@ -27,7 +27,7 @@ FLOPS = 2 * TOKENS * DIM * (2048 + 512 + 512)
 
 ON_TENSOR = {0: (), 1: (3,), 2: (2, 3), 3: (2, 3), 4: (2, 3), 5: (2, 3)}
 ON_SCALAR = {0: (), 1: (), 2: (), 3: (), 4: (), 5: (0, 1)}
-GP_TILES = 2
+GP_TILES = 3
 T_FIRST = False
 E_LATE = False
 
@@ -167,11 +167,11 @@ def tile_attention_pa_kernel(
             return planes[(c, g)] if 1 <= c <= 4 else wkv_raw[(c, g)]
 
         def new_grouped(c, g):
-            gr = work.tile(
-                [P, PACK * NCH], BF16, name="gr%d_%d" % (c, g), tag="gr%d" % ((4 * c + g) % 8), align_bytes=64
-            )
-            grouped[(c, g)] = gr
-            return gr
+            if (c, g) not in grouped:
+                grouped[(c, g)] = work.tile(
+                    [P, PACK * NCH], BF16, name="gr%d_%d" % (c, g), tag="gr%d" % ((4 * c + g) % 8), align_bytes=64
+                )
+            return grouped[(c, g)]
 
         def interleave(eng_copy, c, g):
             gr = new_grouped(c, g)
@@ -196,10 +196,17 @@ def tile_attention_pa_kernel(
                     )
                 il_banks[(c, g, h)] = bank
 
+        def shared(c, g):
+            return c >= 2 and g == ON_TENSOR[c][-1]
+
         def evacuate(c, g):
             words = new_grouped(c, g)[:].bitcast(F32)
-            for h in range(2):
+            for h in range(1 if shared(c, g) else 2):
                 nc.scalar.copy(out=words[:, h * NCH : (h + 1) * NCH], in_=il_banks[(c, g, h)][:].bitcast(F32))
+
+        def evacuate_on_vector(c, g):
+            words = new_grouped(c, g)[:].bitcast(F32)
+            nc.vector.tensor_copy(out=words[:, NCH : 2 * NCH], in_=il_banks[(c, g, 1)][:].bitcast(F32))
 
         def quantize_w(c, g):
             if g == first_quantized[c]:
@@ -270,8 +277,11 @@ def tile_attention_pa_kernel(
                 in1=table[:, m, :, :].unsqueeze(2).to_broadcast([P, 2, heads, HD]),
                 op=MULT,
             )
-            if m < GP_TILES:
+            if m < gp_tiles(c):
                 add(nc.gpsimd, c, m, m + 1)
+
+        def gp_tiles(c):
+            return GP_TILES if c < 4 else 2
 
         def copy_v(m):
             r = work.tile([P, NCH], F32, name="rv%d" % m, tag="rv%d" % m)
@@ -314,8 +324,10 @@ def tile_attention_pa_kernel(
         for c in range(2, CHUNKS):
             v_list += rope(c - 2) + vector_prep(c)
         v_list += rope(4)
+        for c in range(2, CHUNKS):
+            v_list.insert(v_list.index(("RP", c - 2, ROW_TILES - 1)) + 1, ("EV", c, ON_TENSOR[c][-1]))
         for i in range(len(v_list) - 1):
-            if v_list[i][0] == "RA" and v_list[i - 1][0] == "RP":
+            if v_list[i][0] == "RA" and v_list[i - 1][0] in ("RP", "EV"):
                 v_list[i], v_list[i + 1] = v_list[i + 1], v_list[i]
 
         s_list = []
@@ -354,15 +366,19 @@ def tile_attention_pa_kernel(
                 out += [("TX", 0, g)] if c == 2 else ([maker(c - 2, g)] if c > 2 else [])
             if kind in ("IV", "IS", "IL") and 1 <= c <= 4:
                 out.append(("W", c, g))
-            if kind in ("IV", "IS", "E") and c >= 2:
+            if kind in ("IV", "IS", "E", "EV") and c >= 2:
                 out.append(("Q", c - 2, g))
             if kind == "IL":
                 k = tensor_passes.index((c, g))
                 out.append(("XE", 0, 2 + k) if k < 2 else ("E",) + tensor_passes[k - 2])
-            if kind == "E":
+                if k >= 2 and shared(tensor_passes[k - 2][0], tensor_passes[k - 2][1]):
+                    out.append(("EV",) + tensor_passes[k - 2])
+            if kind in ("E", "EV"):
                 out.append(("IL", c, g))
             if kind == "Q":
                 out.append(grouper(c, g))
+                if g in ON_TENSOR[c] and shared(c, g):
+                    out.append(("EV", c, g))
                 if c >= 3:
                     out.append(("MT", c - 3, ROW_TILES - 1))
             if kind == "XE":
@@ -374,7 +390,7 @@ def tile_attention_pa_kernel(
                 out.append(("XE", 0, g // 2) if c == 0 else ("RP", c - 1, g))
             if kind == "MP":
                 out += [("Q", c, quant_order[c][g])] + [("QX", 0, m) for m in range(ROW_TILES)]
-                out += [("E",) + p for p in tensor_passes[-2:]]
+                out += [("E",) + p for p in tensor_passes[-2:]] + [("EV",) + tensor_passes[-1]]
             if kind == "RP":
                 out += [("MT", c, g), ("SIN", 0, 0)]
             if kind == "RA":
@@ -395,6 +411,8 @@ def tile_attention_pa_kernel(
                 tensor_interleave(c, g)
             elif kind == "E":
                 evacuate(c, g)
+            elif kind == "EV":
+                evacuate_on_vector(c, g)
             elif kind == "Q":
                 quantize_w(c, g)
             elif kind == "TX":
@@ -410,7 +428,7 @@ def tile_attention_pa_kernel(
             elif kind == "RP":
                 products(c, g)
             elif kind == "RA":
-                add(nc.vector, c, GP_TILES, ROW_TILES)
+                add(nc.vector, c, gp_tiles(c), ROW_TILES)
             elif kind == "VE":
                 copy_v(g)
             else:

@@ -36,13 +36,13 @@ def tile_attention_pa_kernel(
     tc, x, wq_bytes, wq_scale, wk, wv, freqs_cos, freqs_sin, out_0, out_1, out_2
 ):
     nc = tc.nc
-    x_rows = x.rearrange("b s k -> (b s) k")
+    x_rows = x[0].rearrange("(p m) k -> m p k", m=ROW_TILES)
     wq_view = wq_bytes.rearrange("(g p t) n -> g p t n", p=P, t=PACK)
     wk_view = wk.rearrange("(g p t) n -> g p t n", p=P, t=PACK)
     wv_view = wv.rearrange("(g p t) n -> g p t n", p=P, t=PACK)
-    q_out = out_0.rearrange("b s h d -> (b s) (h d)")
-    k_out = out_1.rearrange("b s h d -> (b s) (h d)")
-    v_out = out_2.rearrange("b s h d -> (b s) (h d)")
+    q_out = out_0[0].rearrange("(p m) h d -> m p (h d)", m=ROW_TILES)
+    k_out = out_1[0].rearrange("(p m) h d -> m p (h d)", m=ROW_TILES)
+    v_out = out_2[0].rearrange("(p m) h d -> m p (h d)", m=ROW_TILES)
 
     with ExitStack() as ctx:
         const = ctx.enter_context(tc.tile_pool(name="const", bufs=1))
@@ -54,10 +54,6 @@ def tile_attention_pa_kernel(
 
         wsc = const.tile([P, PASSES, PACK], F32, name="wsc", tag="wsc")
         nc.scalar.dma_start(out=wsc[:], in_=wq_scale.rearrange("(g p t) o -> p g (t o)", p=P, t=PACK))
-        cos_t = const.tile([P, ROW_TILES, HD // 2], BF16, name="cos_t", tag="cos_t")
-        nc.scalar.dma_start(out=cos_t[:], in_=freqs_cos.rearrange("(m p) i -> p m i", p=P))
-        sin_t = const.tile([P, ROW_TILES, HD // 2], BF16, name="sin_t", tag="sin_t")
-        nc.scalar.dma_start(out=sin_t[:], in_=freqs_sin.rearrange("(m p) i -> p m i", p=P))
 
         wq_b = {}
         wkv_raw = {}
@@ -76,7 +72,7 @@ def tile_attention_pa_kernel(
 
         def load_x(m):
             t = work.tile([P, DIM], BF16, name="xraw%d" % m, tag="pl%d" % (4 + m))
-            nc.sync.dma_start(out=t[:], in_=x_rows[m * P : (m + 1) * P, :])
+            nc.sync.dma_start(out=t[:], in_=x_rows[m])
             x_raw[m] = t
 
         for i, g in enumerate(ON_TENSOR[1] + tuple(j for j in range(PASSES) if j not in ON_TENSOR[1])):
@@ -84,6 +80,12 @@ def tile_attention_pa_kernel(
             load_kv(0, i)
         for m in range(ROW_TILES):
             load_x(m)
+        angles = const.tile([P, 4, ROW_TILES * HD // 2], BF16, name="angles", tag="angles")
+        cos_rows = freqs_cos.rearrange("(p m) i -> p (m i)", m=ROW_TILES)
+        sin_rows = freqs_sin.rearrange("(p m) i -> p (m i)", m=ROW_TILES)
+        nc.sync.dma_start(out=angles[:, 0, :], in_=cos_rows)
+        nc.sync.dma_start(out=angles[:, 1, :], in_=cos_rows)
+        nc.sync.dma_start(out=angles[:, 2, :], in_=sin_rows)
         for g in range(PASSES):
             load_wq(2, g)
         for g in range(PASSES):
@@ -100,7 +102,7 @@ def tile_attention_pa_kernel(
         warm = const.tile([P, 2], F32, name="warm", tag="warm")
         nc.vector.memset(warm[:, 0:1], 0.0)
         nc.scalar.activation(out=warm[:, 1:2], in_=warm[:, 0:1], func=COPY)
-        table = const.tile([P, ROW_TILES, 2, HD], F32, name="table", tag="table")
+        table = const.tile([P, 2, ROW_TILES, HD], F32, name="table", tag="table")
 
         x_codes = keep.tile([P, ROW_TILES, PASSES * P], U32, name="x_codes", tag="x_codes", align_bytes=64)
         x_scales = keep.tile([P, ROW_TILES, PASSES * P], U8, name="x_scales", tag="x_scales", align_bytes=64)
@@ -125,11 +127,13 @@ def tile_attention_pa_kernel(
             return ("E", c, g) if g in ON_TENSOR[c] else maker(c, g)
 
         def sin_table():
-            pairs = table[:].rearrange("p m a (i e) -> p m a i e", e=2)
-            for e in range(2):
-                nc.vector.tensor_copy(out=pairs[:, :, 0, :, e], in_=cos_t[:])
-            nc.vector.tensor_copy(out=pairs[:, :, 1, :, 0], in_=sin_t[:])
-            nc.vector.tensor_scalar_mul(out=pairs[:, :, 1, :, 1], in0=sin_t[:], scalar1=-1.0)
+            nc.vector.tensor_copy(
+                out=table[:].rearrange("p a m (i e) -> p a (m i) e", e=2),
+                in_=angles[:].rearrange("p (a e) x -> p a x e", e=2),
+            )
+
+        def minus_sin():
+            nc.vector.tensor_scalar_mul(out=angles[:, 3, :], in0=angles[:, 2, :], scalar1=-1.0)
 
         def transpose_x(m):
             words = x_raw[m][:].bitcast(F32)
@@ -243,13 +247,12 @@ def tile_attention_pa_kernel(
                 one_matmul(c, m, g, i == 0, i == PASSES - 1)
 
         def store(c, m, tile_ap, queue=None):
-            rows = slice(m * P, (m + 1) * P)
             if c == 0:
-                dst = k_out[rows, :]
+                dst = k_out[m]
             elif c == 5:
-                dst = v_out[rows, :]
+                dst = v_out[m]
             else:
-                dst = q_out[rows, (c - 1) * NCH : c * NCH]
+                dst = q_out[m, :, (c - 1) * NCH : c * NCH]
             (queue or nc.sync).dma_start(out=dst, in_=tile_ap)
 
         def add(eng, c, m0, m1):
@@ -274,7 +277,7 @@ def tile_attention_pa_kernel(
             nc.vector.tensor_tensor(
                 out=both[:, m, :, :].rearrange("p a (h d) -> p a h d", d=HD),
                 in0=acc[(c, m)][:].rearrange("p (h d) -> p h d", d=HD).unsqueeze(1).to_broadcast([P, 2, heads, HD]),
-                in1=table[:, m, :, :].unsqueeze(2).to_broadcast([P, 2, heads, HD]),
+                in1=table[:, :, m, :].unsqueeze(2).to_broadcast([P, 2, heads, HD]),
                 op=MULT,
             )
             if m < gp_tiles(c):
@@ -315,12 +318,16 @@ def tile_attention_pa_kernel(
         def rope(c):
             return [("RP", c, m) for m in range(ROW_TILES)] + [("RA", c, 0)]
 
-        v_list = vector_prep(0) + [("SIN", 0, 0)]
+        v_list = vector_prep(0)
         prep1 = vector_prep(1)
         for i, step in enumerate(prep1):
             v_list.append(step)
             if i < ROW_TILES:
                 v_list.append(("QX", 0, i))
+            if i == 3:
+                v_list.append(("NEG", 0, 0))
+            if i == 5:
+                v_list.append(("SIN", 0, 0))
         for c in range(2, CHUNKS):
             v_list += rope(c - 2) + vector_prep(c)
         v_list += rope(4)
@@ -395,6 +402,8 @@ def tile_attention_pa_kernel(
                 out += [("MT", c, g), ("SIN", 0, 0)]
             if kind == "RA":
                 out.append(("RP", c, ROW_TILES - 1))
+            if kind == "SIN":
+                out.append(("NEG", 0, 0))
             if kind == "VE":
                 out.append(("MP", 5, PASSES - 1))
             return out
@@ -431,6 +440,8 @@ def tile_attention_pa_kernel(
                 add(nc.vector, c, gp_tiles(c), ROW_TILES)
             elif kind == "VE":
                 copy_v(g)
+            elif kind == "NEG":
+                minus_sin()
             else:
                 sin_table()
 

@@ -84,8 +84,8 @@ def tile_attention_pa_kernel(
         cos_rows = freqs_cos.rearrange("(p m) i -> p (m i)", m=ROW_TILES)
         sin_rows = freqs_sin.rearrange("(p m) i -> p (m i)", m=ROW_TILES)
         nc.sync.dma_start(out=angles[:, 0, :], in_=cos_rows)
-        nc.sync.dma_start(out=angles[:, 1, :], in_=cos_rows)
-        nc.sync.dma_start(out=angles[:, 2, :], in_=sin_rows)
+        nc.sync.dma_start(out=angles[:, 3, :], in_=cos_rows)
+        nc.sync.dma_start(out=angles[:, 1, :], in_=sin_rows)
         for g in range(PASSES):
             load_wq(2, g)
         for g in range(PASSES):
@@ -133,7 +133,7 @@ def tile_attention_pa_kernel(
             )
 
         def minus_sin():
-            nc.vector.tensor_scalar_mul(out=angles[:, 3, :], in0=angles[:, 2, :], scalar1=-1.0)
+            nc.vector.tensor_scalar_mul(out=angles[:, 2, :], in0=angles[:, 1, :], scalar1=-1.0)
 
         def transpose_x(m):
             words = x_raw[m][:].bitcast(F32)
@@ -258,10 +258,7 @@ def tile_attention_pa_kernel(
         def add(eng, c, m0, m1):
             both, r = rot[c]
             eng.tensor_tensor(
-                out=r[:, m0:m1, :].rearrange("p a (j e) -> p a j e", e=2),
-                in0=both[:, m0:m1, 0, :].rearrange("p a (j e) -> p a j e", e=2),
-                in1=both[:, m0:m1, 1, :].rearrange("p a (j e) -> p a j e", e=2)[:, :, :, ::-1],
-                op=ADD,
+                out=r[:, m0:m1, :], in0=both[:, m0:m1, 0, :], in1=both[:, m0:m1, 1, :], op=ADD
             )
             for m in range(m0, m1):
                 store(c, m, r[:, m, :])
@@ -274,10 +271,11 @@ def tile_attention_pa_kernel(
                     work.tile([P, ROW_TILES, NCH], F32, name="r%d" % c, tag="r%d" % (c % 2)),
                 )
             both, r = rot[c]
+            shape = [P, 2, heads, HD // 2, 2]
             nc.vector.tensor_tensor(
-                out=both[:, m, :, :].rearrange("p a (h d) -> p a h d", d=HD),
-                in0=acc[(c, m)][:].rearrange("p (h d) -> p h d", d=HD).unsqueeze(1).to_broadcast([P, 2, heads, HD]),
-                in1=table[:, :, m, :].unsqueeze(2).to_broadcast([P, 2, heads, HD]),
+                out=both[:, m, :, :].rearrange("p a (h i f) -> p a h i f", h=heads, f=2),
+                in0=acc[(c, m)][:].rearrange("p (h i a) -> p a h i", h=heads, a=2).unsqueeze(4).to_broadcast(shape),
+                in1=table[:, :, m, :].rearrange("p a (i f) -> p a i f", f=2).unsqueeze(2).to_broadcast(shape),
                 op=MULT,
             )
             if m < gp_tiles(c):

@@ -21,15 +21,15 @@ PASSES = 4
 NCH = 512
 ROW_TILES = 4
 HD = 128
+HEADS = NCH // HD
 CHUNKS = 6
+KEYS = 0
+VALUES = 5
 
 FLOPS = 2 * TOKENS * DIM * (2048 + 512 + 512)
 
 ON_TENSOR = {0: (), 1: (3,), 2: (2, 3), 3: (2, 3), 4: (2, 3), 5: (2, 3)}
 ON_SCALAR = {0: (), 1: (), 2: (), 3: (), 4: (), 5: (0, 1)}
-GP_TILES = 3
-T_FIRST = False
-E_LATE = False
 
 
 def tile_attention_pa_kernel(
@@ -65,19 +65,18 @@ def tile_attention_pa_kernel(
             wq_b[(c, g)] = t
 
         def load_kv(c, g):
-            view = wk_view if c == 0 else wv_view
+            view = wk_view if c == KEYS else wv_view
             t = raw.tile([P, PACK, NCH], BF16, name="wkv%d_%d" % (c, g), tag="wkv%d_%d" % (c, g))
             nc.sync.dma_start(out=t[:], in_=view[g])
             wkv_raw[(c, g)] = t
 
         def load_x(m):
-            t = work.tile([P, DIM], BF16, name="xraw%d" % m, tag="pl%d" % (4 + m))
-            nc.sync.dma_start(out=t[:], in_=x_rows[m])
-            x_raw[m] = t
+            x_raw[m] = work.tile([P, DIM], BF16, name="xraw%d" % m, tag="pl%d" % (4 + m))
+            nc.sync.dma_start(out=x_raw[m][:], in_=x_rows[m])
 
-        for i, g in enumerate(ON_TENSOR[1] + tuple(j for j in range(PASSES) if j not in ON_TENSOR[1])):
+        for i, g in enumerate((3, 0, 1, 2)):
             load_wq(1, g)
-            load_kv(0, i)
+            load_kv(KEYS, i)
         for m in range(ROW_TILES):
             load_x(m)
         angles = const.tile([P, 4, ROW_TILES * HD // 2], BF16, name="angles", tag="angles")
@@ -91,7 +90,7 @@ def tile_attention_pa_kernel(
         for g in range(PASSES):
             load_wq(3, g)
         for g in range(PASSES):
-            load_kv(5, g)
+            load_kv(VALUES, g)
         for g in range(PASSES):
             load_wq(4, g)
 
@@ -114,26 +113,23 @@ def tile_attention_pa_kernel(
         x_grouped = {}
         il_banks = {}
         acc = {}
-        rot = {}
-
+        both = {}
         tensor_passes = [(c, g) for c in range(CHUNKS) for g in ON_TENSOR[c]]
 
-        def maker(c, g):
-            if g in ON_TENSOR[c]:
-                return ("IL", c, g)
-            return ("IS", c, g) if g in ON_SCALAR[c] else ("IV", c, g)
+        def deferred(c, m):
+            return m == 2 and c <= 3
 
-        def grouper(c, g):
-            return ("E", c, g) if g in ON_TENSOR[c] else maker(c, g)
+        def widened(c):
+            return KEYS < c < VALUES
+
+        def minus_sin():
+            nc.vector.tensor_scalar_mul(out=angles[:, 2, :], in0=angles[:, 1, :], scalar1=-1.0)
 
         def sin_table():
             nc.vector.tensor_copy(
                 out=table[:].rearrange("p a m (i e) -> p a (m i) e", e=2),
                 in_=angles[:].rearrange("p (a e) x -> p a x e", e=2),
             )
-
-        def minus_sin():
-            nc.vector.tensor_scalar_mul(out=angles[:, 2, :], in0=angles[:, 1, :], scalar1=-1.0)
 
         def transpose_x(m):
             words = x_raw[m][:].bitcast(F32)
@@ -147,28 +143,31 @@ def tile_attention_pa_kernel(
                 x_banks[(m, h)] = bank
 
         def copy_x(m):
-            xg = work.tile([P, DIM], BF16, name="xg%d" % m, tag="xg%d" % m, align_bytes=64)
-            xg_words = xg[:].bitcast(F32)
+            x_grouped[m] = work.tile([P, DIM], BF16, name="xg%d" % m, tag="xg%d" % m, align_bytes=64)
+            xg_words = x_grouped[m][:].bitcast(F32)
             for h in range(2):
                 nc.scalar.copy(
                     out=xg_words[:, 512 * h : 512 * (h + 1)].rearrange("p (g r u) -> p g r u", g=2, u=2),
                     in_=x_banks[(m, h)][:].rearrange("p (g u r) -> p g r u", g=2, u=2),
                 )
-            x_grouped[m] = xg
 
         def quantize_x(m):
             nc.vector.quantize_mx(out=x_codes[:, m, :].bitcast(FP8X4), scales=x_scales[:, m, :], in_=x_grouped[m][:])
 
         def widen(c, g):
-            pl = work.tile([P, PACK, NCH], BF16, name="pl%d_%d" % (c, g), tag="pl%d" % ((4 * (c - 1) + g) % 8))
+            planes[(c, g)] = work.tile(
+                [P, PACK, NCH], BF16, name="pl%d_%d" % (c, g), tag="pl%d" % ((4 * (c - 1) + g) % 8)
+            )
             for t in range(PACK):
                 nc.scalar.activation(
-                    out=pl[:, t, :], in_=wq_b[(c, g)][:, t, :].bitcast(FP8), func=COPY, scale=wsc[:, g, t : t + 1]
+                    out=planes[(c, g)][:, t, :],
+                    in_=wq_b[(c, g)][:, t, :].bitcast(FP8),
+                    func=COPY,
+                    scale=wsc[:, g, t : t + 1],
                 )
-            planes[(c, g)] = pl
 
         def source(c, g):
-            return planes[(c, g)] if 1 <= c <= 4 else wkv_raw[(c, g)]
+            return planes[(c, g)] if widened(c) else wkv_raw[(c, g)]
 
         def new_grouped(c, g):
             if (c, g) not in grouped:
@@ -178,9 +177,8 @@ def tile_attention_pa_kernel(
             return grouped[(c, g)]
 
         def interleave(eng_copy, c, g):
-            gr = new_grouped(c, g)
             eng_copy(
-                out=gr[:].rearrange("p (c i t) -> p c t i", i=4, t=PACK),
+                out=new_grouped(c, g)[:].rearrange("p (c i t) -> p c t i", i=4, t=PACK),
                 in_=source(c, g)[:].rearrange("p t (c i) -> p c t i", i=4),
             )
 
@@ -200,20 +198,12 @@ def tile_attention_pa_kernel(
                     )
                 il_banks[(c, g, h)] = bank
 
-        def shared(c, g):
-            return c >= 2 and g == ON_TENSOR[c][-1]
-
-        def evacuate(c, g):
+        def evacuate(eng_copy, c, g, h):
             words = new_grouped(c, g)[:].bitcast(F32)
-            for h in range(1 if shared(c, g) else 2):
-                nc.scalar.copy(out=words[:, h * NCH : (h + 1) * NCH], in_=il_banks[(c, g, h)][:].bitcast(F32))
-
-        def evacuate_on_vector(c, g):
-            words = new_grouped(c, g)[:].bitcast(F32)
-            nc.vector.tensor_copy(out=words[:, NCH : 2 * NCH], in_=il_banks[(c, g, 1)][:].bitcast(F32))
+            eng_copy(out=words[:, h * NCH : (h + 1) * NCH], in_=il_banks[(c, g, h)][:].bitcast(F32))
 
         def quantize_w(c, g):
-            if g == first_quantized[c]:
+            if c not in w_codes:
                 w_codes[c] = keep.tile(
                     [P, PASSES, NCH], U32, name="w_codes%d" % c, tag="w_codes%d" % (c % 3), align_bytes=64
                 )
@@ -241,149 +231,119 @@ def tile_attention_pa_kernel(
             for g in range(PASSES):
                 one_matmul(c, m, g, g == 0, g == PASSES - 1)
 
-        def multiply_pass(c, i):
-            g = quant_order[c][i]
+        def multiply_pass(c, g):
             for m in range(ROW_TILES):
-                one_matmul(c, m, g, i == 0, i == PASSES - 1)
+                one_matmul(c, m, g, g == 0, g == PASSES - 1)
 
-        def store(c, m, tile_ap, queue=None):
-            if c == 0:
+        def store(queue, c, m, tile_ap):
+            if c == KEYS:
                 dst = k_out[m]
-            elif c == 5:
+            elif c == VALUES:
                 dst = v_out[m]
             else:
                 dst = q_out[m, :, (c - 1) * NCH : c * NCH]
-            (queue or nc.sync).dma_start(out=dst, in_=tile_ap)
-
-        def add(eng, c, m0, m1):
-            both, r = rot[c]
-            eng.tensor_tensor(
-                out=r[:, m0:m1, :], in0=both[:, m0:m1, 0, :], in1=both[:, m0:m1, 1, :], op=ADD
-            )
-            for m in range(m0, m1):
-                store(c, m, r[:, m, :])
+            queue.dma_start(out=dst, in_=tile_ap)
 
         def products(c, m):
-            heads = NCH // HD
-            if m == 0:
-                rot[c] = (
-                    work.tile([P, ROW_TILES, 2, NCH], F32, name="both%d" % c, tag="both"),
-                    work.tile([P, ROW_TILES, NCH], F32, name="r%d" % c, tag="r%d" % (c % 2)),
-                )
-            both, r = rot[c]
-            shape = [P, 2, heads, HD // 2, 2]
+            both[(c, m)] = work.tile([P, 2, NCH], F32, name="both%d_%d" % (c, m), tag="both%d" % m)
+            shape = [P, 2, HEADS, HD // 2, 2]
             nc.vector.tensor_tensor(
-                out=both[:, m, :, :].rearrange("p a (h i f) -> p a h i f", h=heads, f=2),
-                in0=acc[(c, m)][:].rearrange("p (h i a) -> p a h i", h=heads, a=2).unsqueeze(4).to_broadcast(shape),
+                out=both[(c, m)][:].rearrange("p a (h i f) -> p a h i f", h=HEADS, f=2),
+                in0=acc[(c, m)][:].rearrange("p (h i a) -> p a h i", h=HEADS, a=2).unsqueeze(4).to_broadcast(shape),
                 in1=table[:, :, m, :].rearrange("p a (i f) -> p a i f", f=2).unsqueeze(2).to_broadcast(shape),
                 op=MULT,
             )
-            if m < gp_tiles(c):
-                add(nc.gpsimd, c, m, m + 1)
 
-        def gp_tiles(c):
-            return GP_TILES if c < 4 else 2
+        def add(eng, c, m):
+            tag = "gr%d" % ((4 * c + 3) % 8) if deferred(c, m) else "r%d_%d" % (m, c % 2)
+            if deferred(c, m):
+                r = work.tile([P, NCH], F32, name="r%d_%d" % (c, m), tag=tag, align_bytes=64)
+            else:
+                r = work.tile([P, NCH], F32, name="r%d_%d" % (c, m), tag=tag)
+            eng.tensor_tensor(out=r[:], in0=both[(c, m)][:, 0, :], in1=both[(c, m)][:, 1, :], op=ADD)
+            store(nc.sync, c, m, r[:])
+
+        v_rows = {}
 
         def copy_v(m):
-            r = work.tile([P, NCH], F32, name="rv%d" % m, tag="rv%d" % m)
-            nc.scalar.copy(out=r[:], in_=acc[(5, m)][:])
-            store(5, m, r[:], nc.scalar)
+            v_rows[m] = work.tile([P, NCH], F32, name="rv%d" % m, tag="rv%d" % m)
+            nc.scalar.copy(out=v_rows[m][:], in_=acc[(VALUES, m)][:])
 
-        on_vector = {c: tuple(g for g in range(PASSES) if g not in ON_TENSOR[c] + ON_SCALAR[c]) for c in range(CHUNKS)}
-        others = {c: ON_SCALAR[c] + ON_TENSOR[c] for c in range(CHUNKS)}
-        quant_order = {c: (others[c] + on_vector[c]) if T_FIRST else (on_vector[c] + others[c]) for c in range(CHUNKS)}
-        widen_order = {c: (ON_TENSOR[c] + on_vector[c] + ON_SCALAR[c]) if T_FIRST else (on_vector[c] + others[c]) for c in range(CHUNKS)}
-        first_quantized = {c: quant_order[c][0] for c in range(CHUNKS)}
+        def store_v(m):
+            store(nc.scalar, VALUES, m, v_rows[m][:])
 
-        def vector_prep(c):
-            seq = []
-            if T_FIRST:
-                for j, g in enumerate(on_vector[c]):
-                    seq.append(("IV", c, g))
-                    if j < len(others[c]):
-                        seq.append(("Q", c, others[c][j]))
-                seq += [("Q", c, g) for g in others[c][len(on_vector[c]) :]]
-                seq += [("Q", c, g) for g in on_vector[c]]
-            else:
-                for j, g in enumerate(on_vector[c]):
-                    seq.append(("IV", c, g))
-                    if j >= 1:
-                        seq.append(("Q", c, on_vector[c][j - 1]))
-                seq += [("Q", c, g) for g in on_vector[c][-1:]]
-                seq += [("Q", c, g) for g in others[c]]
-            return seq
+        v_list = [
+            ("IV", 0, 0), ("IV", 0, 1), ("Q", 0, 0), ("IV", 0, 2), ("Q", 0, 1), ("IV", 0, 3), ("Q", 0, 2), ("Q", 0, 3),
+            ("IV", 1, 0), ("QX", 0, 0), ("IV", 1, 1), ("QX", 0, 1), ("Q", 1, 0), ("QX", 0, 2), ("IV", 1, 2), ("QX", 0, 3),
+            ("NEG", 0, 0), ("Q", 1, 1), ("Q", 1, 2), ("SIN", 0, 0), ("Q", 1, 3),
+        ]
+        for c in range(2, VALUES):
+            v_list += [("RP", c - 2, m) for m in range(ROW_TILES)]
+            v_list += [("EV", c, (3, 1)), ("IV", c, 0), ("RA", c - 2, 3), ("IV", c, 1)]
+            v_list += [("Q", c, g) for g in range(PASSES)]
+        v_list += [("RP", 3, m) for m in range(ROW_TILES)]
+        v_list += [("Q", VALUES, 0), ("RA", 3, 3), ("Q", VALUES, 1), ("Q", VALUES, 2), ("Q", VALUES, 3)]
+        v_list += [("RP", 4, m) for m in range(ROW_TILES)] + [("RA", 4, 2), ("RA", 4, 3)]
 
-        def rope(c):
-            return [("RP", c, m) for m in range(ROW_TILES)] + [("RA", c, 0)]
+        g_list = []
+        for c in range(5):
+            if c > 0:
+                g_list.append(("GA", c - 1, 2))
+            g_list += [("GA", c, 0), ("GA", c, 1)]
 
-        v_list = vector_prep(0)
-        prep1 = vector_prep(1)
-        for i, step in enumerate(prep1):
-            v_list.append(step)
-            if i < ROW_TILES:
-                v_list.append(("QX", 0, i))
-            if i == 3:
-                v_list.append(("NEG", 0, 0))
-            if i == 5:
-                v_list.append(("SIN", 0, 0))
-        for c in range(2, CHUNKS):
-            v_list += rope(c - 2) + vector_prep(c)
-        v_list += rope(4)
-        for c in range(2, CHUNKS):
-            v_list.insert(v_list.index(("RP", c - 2, ROW_TILES - 1)) + 1, ("EV", c, ON_TENSOR[c][-1]))
-        for i in range(len(v_list) - 1):
-            if v_list[i][0] == "RA" and v_list[i - 1][0] in ("RP", "EV"):
-                v_list[i], v_list[i + 1] = v_list[i + 1], v_list[i]
-
-        s_list = []
-        waiting = []
-        for c in range(1, 5):
-            for g in ON_TENSOR[c] + on_vector[c] + ON_SCALAR[c]:
-                s_list.append(("W", c, g))
-                if E_LATE and c > 1:
-                    s_list += waiting[:1]
-                    waiting = waiting[1:]
-                if g in ON_SCALAR[c]:
-                    s_list.append(("IS", c, g))
-            if c == 1:
-                s_list += [("XE", 0, m) for m in range(ROW_TILES)]
-            s_list += waiting
-            waiting = [("E", c, g) for g in ON_TENSOR[c]]
-            if not E_LATE:
-                s_list += waiting
-                waiting = []
-        for g in ON_SCALAR[5]:
-            s_list.append(("IS", 5, g))
-            s_list += waiting[:1]
-            waiting = waiting[1:]
-        s_list += waiting + [("E", 5, g) for g in ON_TENSOR[5]] + [("VE", 5, m) for m in range(ROW_TILES)]
+        s_list = [("W", 1, g) for g in (3, 0, 1, 2)] + [("XE", 0, m) for m in range(ROW_TILES)]
+        s_list += [("E", 1, (3, 0)), ("E", 1, (3, 1))]
+        for c in range(2, VALUES):
+            s_list += [("W", c, g) for g in (2, 3, 0, 1)]
+            s_list += [("E", c, (2, 0)), ("E", c, (2, 1)), ("E", c, (3, 0))]
+        s_list += [("IS", VALUES, g) for g in ON_SCALAR[VALUES]]
+        s_list += [("E", VALUES, (g, h)) for g in ON_TENSOR[VALUES] for h in range(2)]
+        for m in range(ROW_TILES):
+            s_list.append(("VE", 5, m))
+            if m > 0:
+                s_list.append(("VS", 5, m - 1))
+        s_list.append(("VS", 5, ROW_TILES - 1))
 
         t_list = [("TX", 0, m) for m in range(ROW_TILES)] + [("IL", 1, g) for g in ON_TENSOR[1]]
         t_list += [("MT", 0, m) for m in range(ROW_TILES)]
-        for c in range(1, 5):
+        for c in range(1, VALUES):
             t_list += [("IL", c + 1, g) for g in ON_TENSOR[c + 1]] + [("MT", c, m) for m in range(ROW_TILES)]
-        t_list += [("MP", 5, i) for i in range(PASSES)]
+        t_list += [("MP", VALUES, g) for g in range(PASSES)]
+
+        lists = [s_list, v_list, t_list, g_list]
+        steps = set(s_list + v_list + t_list + g_list)
+
+        def empties(c, g):
+            return [(k, c, (g, h)) for h in range(2) for k in ("E", "EV") if (k, c, (g, h)) in steps]
+
+        def interleaver(c, g):
+            if g in ON_TENSOR[c]:
+                return ("IL", c, g)
+            return ("IS" if g in ON_SCALAR[c] else "IV", c, g)
 
         def needs(step):
             kind, c, g = step
             out = []
             if kind == "W":
-                out += [("TX", 0, g)] if c == 2 else ([maker(c - 2, g)] if c > 2 else [])
-            if kind in ("IV", "IS", "IL") and 1 <= c <= 4:
+                if c == 2:
+                    out.append(("TX", 0, g))
+                elif c > 2:
+                    out.append(interleaver(c - 2, g))
+            if kind in ("IV", "IS", "IL") and widened(c):
                 out.append(("W", c, g))
-            if kind in ("IV", "IS", "E", "EV") and c >= 2:
-                out.append(("Q", c - 2, g))
+            if kind in ("IV", "IS", "E", "EV"):
+                p = g[0] if kind in ("E", "EV") else g
+                if c >= 2:
+                    out.append(("Q", c - 2, p))
+                if c >= 4 and p == 3:
+                    out.append(("GA", c - 4, 2))
+            if kind in ("E", "EV"):
+                out.append(("IL", c, g[0]))
             if kind == "IL":
                 k = tensor_passes.index((c, g))
-                out.append(("XE", 0, 2 + k) if k < 2 else ("E",) + tensor_passes[k - 2])
-                if k >= 2 and shared(tensor_passes[k - 2][0], tensor_passes[k - 2][1]):
-                    out.append(("EV",) + tensor_passes[k - 2])
-            if kind in ("E", "EV"):
-                out.append(("IL", c, g))
+                out += [("XE", 0, 2 + k)] if k < 2 else empties(tensor_passes[k - 2][0], tensor_passes[k - 2][1])
             if kind == "Q":
-                out.append(grouper(c, g))
-                if g in ON_TENSOR[c] and shared(c, g):
-                    out.append(("EV", c, g))
+                out += empties(c, g) if g in ON_TENSOR[c] else [interleaver(c, g)]
                 if c >= 3:
                     out.append(("MT", c - 3, ROW_TILES - 1))
             if kind == "XE":
@@ -391,67 +351,57 @@ def tile_attention_pa_kernel(
             if kind == "QX":
                 out.append(("XE", 0, g))
             if kind == "MT":
-                out += [("Q", c, j) for j in range(PASSES)] + [("QX", 0, g)]
+                out += [("Q", c, p) for p in range(PASSES)] + [("QX", 0, g)]
                 out.append(("XE", 0, g // 2) if c == 0 else ("RP", c - 1, g))
             if kind == "MP":
-                out += [("Q", c, quant_order[c][g])] + [("QX", 0, m) for m in range(ROW_TILES)]
-                out += [("E",) + p for p in tensor_passes[-2:]] + [("EV",) + tensor_passes[-1]]
+                out.append(("Q", c, g))
+                for p in tensor_passes[-2:]:
+                    out += empties(p[0], p[1])
             if kind == "RP":
                 out += [("MT", c, g), ("SIN", 0, 0)]
-            if kind == "RA":
-                out.append(("RP", c, ROW_TILES - 1))
+                if c > 0:
+                    out.append(("GA" if ("GA", c - 1, g) in steps else "RA", c - 1, g))
+            if kind in ("RA", "GA"):
+                out.append(("RP", c, g))
+                if deferred(c, g):
+                    out.append(("Q", c + 2, 3))
+            if kind == "VE":
+                out.append(("MP", VALUES, PASSES - 1))
             if kind == "SIN":
                 out.append(("NEG", 0, 0))
-            if kind == "VE":
-                out.append(("MP", 5, PASSES - 1))
             return out
 
-        def emit(step):
-            kind, c, g = step
-            if kind == "W":
-                widen(c, g)
-            elif kind == "IV":
-                interleave(nc.vector.tensor_copy, c, g)
-            elif kind == "IS":
-                interleave(nc.scalar.copy, c, g)
-            elif kind == "IL":
-                tensor_interleave(c, g)
-            elif kind == "E":
-                evacuate(c, g)
-            elif kind == "EV":
-                evacuate_on_vector(c, g)
-            elif kind == "Q":
-                quantize_w(c, g)
-            elif kind == "TX":
-                transpose_x(g)
-            elif kind == "XE":
-                copy_x(g)
-            elif kind == "QX":
-                quantize_x(g)
-            elif kind == "MT":
-                multiply_tile(c, g)
-            elif kind == "MP":
-                multiply_pass(c, g)
-            elif kind == "RP":
-                products(c, g)
-            elif kind == "RA":
-                add(nc.vector, c, gp_tiles(c), ROW_TILES)
-            elif kind == "VE":
-                copy_v(g)
-            elif kind == "NEG":
-                minus_sin()
-            else:
-                sin_table()
+        emitters = {
+            "W": widen,
+            "IV": lambda c, g: interleave(nc.vector.tensor_copy, c, g),
+            "IS": lambda c, g: interleave(nc.scalar.copy, c, g),
+            "IL": tensor_interleave,
+            "E": lambda c, g: evacuate(nc.scalar.copy, c, g[0], g[1]),
+            "EV": lambda c, g: evacuate(nc.vector.tensor_copy, c, g[0], g[1]),
+            "Q": quantize_w,
+            "TX": lambda c, m: transpose_x(m),
+            "XE": lambda c, m: copy_x(m),
+            "QX": lambda c, m: quantize_x(m),
+            "MT": multiply_tile,
+            "MP": multiply_pass,
+            "RP": products,
+            "RA": lambda c, m: add(nc.vector, c, m),
+            "GA": lambda c, m: add(nc.gpsimd, c, m),
+            "VE": lambda c, m: copy_v(m),
+            "VS": lambda c, m: store_v(m),
+            "NEG": lambda c, m: minus_sin(),
+            "SIN": lambda c, m: sin_table(),
+        }
 
-        lists = [s_list, v_list, t_list]
-        at = [0, 0, 0]
+        at = [0, 0, 0, 0]
         done = set()
-        while any(at[i] < len(lists[i]) for i in range(3)):
+        while any(at[i] < len(lists[i]) for i in range(4)):
             moved = False
-            for i in range(3):
+            for i in range(4):
                 while at[i] < len(lists[i]) and all(n in done for n in needs(lists[i][at[i]])):
-                    emit(lists[i][at[i]])
+                    kind, c, g = lists[i][at[i]]
+                    emitters[kind](c, g)
                     done.add(lists[i][at[i]])
                     at[i] += 1
                     moved = True
-            assert moved, "the three orders wait for each other"
+            assert moved, "the four orders wait for each other"

@@ -28,8 +28,8 @@ VALUES = 5
 
 FLOPS = 2 * TOKENS * DIM * (2048 + 512 + 512)
 
-ON_TENSOR = {0: (), 1: (3,), 2: (2, 3), 3: (2, 3), 4: (2, 3), 5: (2, 3)}
-ON_SCALAR = {0: (), 1: (), 2: (), 3: (), 4: (), 5: (0, 1)}
+ON_TENSOR = {0: (), 1: (3,), 2: (2, 3), 3: (2, 3), 4: (2, 3), 5: ()}
+ON_SCALAR = {0: (), 1: (), 2: (), 3: (), 4: (), 5: (0, 1, 2, 3)}
 
 
 def tile_attention_pa_kernel(
@@ -216,7 +216,7 @@ def tile_attention_pa_kernel(
 
         def one_matmul(c, m, g, first, last):
             if first:
-                acc[(c, m)] = psum.tile([P, NCH], F32, name="acc%d_%d" % (c, m), tag="b%d" % (m if c < 5 else 4 + m))
+                acc[(c, m)] = psum.tile([P, NCH], F32, name="acc%d_%d" % (c, m), tag="b%d" % (4 + m if c == 4 else m))
             nc.tensor.matmul_mx(
                 out=acc[(c, m)][:],
                 lhsT=x_codes[:, m, g * P : (g + 1) * P].bitcast(FP8X4),
@@ -297,7 +297,6 @@ def tile_attention_pa_kernel(
             s_list += [("W", c, g) for g in (2, 3, 0, 1)]
             s_list += [("E", c, (2, 0)), ("E", c, (2, 1)), ("E", c, (3, 0))]
         s_list += [("IS", VALUES, g) for g in ON_SCALAR[VALUES]]
-        s_list += [("E", VALUES, (g, h)) for g in ON_TENSOR[VALUES] for h in range(2)]
         for m in range(ROW_TILES):
             s_list.append(("VE", 5, m))
             if m > 0:
@@ -352,11 +351,12 @@ def tile_attention_pa_kernel(
                 out.append(("XE", 0, g))
             if kind == "MT":
                 out += [("Q", c, p) for p in range(PASSES)] + [("QX", 0, g)]
-                out.append(("XE", 0, g // 2) if c == 0 else ("RP", c - 1, g))
+                if c == 4:
+                    out += empties(4, 2) + empties(4, 3)
+                else:
+                    out.append(("XE", 0, g // 2) if c == 0 else ("RP", c - 1, g))
             if kind == "MP":
-                out.append(("Q", c, g))
-                for p in tensor_passes[-2:]:
-                    out += empties(p[0], p[1])
+                out += [("Q", c, g)] + [("RP", 3, m) for m in range(ROW_TILES)]
             if kind == "RP":
                 out += [("MT", c, g), ("SIN", 0, 0)]
                 if c > 0:

@@ -28,6 +28,8 @@ VALUES = 5
 
 FLOPS = 2 * TOKENS * DIM * (2048 + 512 + 512)
 
+X_BANKS = (0, 2, 6, 0)
+
 ON_TENSOR = {0: (), 1: (3,), 2: (2, 3), 3: (2, 3), 4: (2, 3), 5: ()}
 ON_SCALAR = {0: (), 1: (), 2: (), 3: (), 4: (), 5: (0, 1, 2, 3)}
 
@@ -134,7 +136,7 @@ def tile_attention_pa_kernel(
         def transpose_x(m):
             words = x_raw[m][:].bitcast(F32)
             for h in range(2):
-                bank = psum.tile([P, 512], F32, name="xt%d_%d" % (m, h), tag="b%d" % (2 * m + h))
+                bank = psum.tile([P, 512], F32, name="xt%d_%d" % (m, h), tag="b%d" % (X_BANKS[m] + h))
                 for gl in range(2):
                     g = 2 * h + gl
                     for u in range(2):
@@ -303,7 +305,7 @@ def tile_attention_pa_kernel(
                 s_list.append(("VS", 5, m - 1))
         s_list.append(("VS", 5, ROW_TILES - 1))
 
-        t_list = [("TX", 0, m) for m in range(ROW_TILES)] + [("IL", 1, g) for g in ON_TENSOR[1]]
+        t_list = [("IL", 1, g) for g in ON_TENSOR[1]] + [("TX", 0, m) for m in range(ROW_TILES)]
         t_list += [("MT", 0, m) for m in range(ROW_TILES)]
         for c in range(1, VALUES):
             t_list += [("IL", c + 1, g) for g in ON_TENSOR[c + 1]] + [("MT", c, m) for m in range(ROW_TILES)]
@@ -340,11 +342,13 @@ def tile_attention_pa_kernel(
                 out.append(("IL", c, g[0]))
             if kind == "IL":
                 k = tensor_passes.index((c, g))
-                out += [("XE", 0, 2 + k)] if k < 2 else empties(tensor_passes[k - 2][0], tensor_passes[k - 2][1])
+                out += ([], [("XE", 0, 2)])[k] if k < 2 else empties(tensor_passes[k - 2][0], tensor_passes[k - 2][1])
             if kind == "Q":
                 out += empties(c, g) if g in ON_TENSOR[c] else [interleaver(c, g)]
                 if c >= 3:
                     out.append(("MT", c - 3, ROW_TILES - 1))
+            if kind == "TX" and g == 3:
+                out.append(("XE", 0, 0))
             if kind == "XE":
                 out.append(("TX", 0, g))
             if kind == "QX":
@@ -354,7 +358,7 @@ def tile_attention_pa_kernel(
                 if c == 4:
                     out += empties(4, 2) + empties(4, 3)
                 else:
-                    out.append(("XE", 0, g // 2) if c == 0 else ("RP", c - 1, g))
+                    out.append(("XE", 0, (3, 3, 1, 1)[g]) if c == 0 else ("RP", c - 1, g))
             if kind == "MP":
                 out += [("Q", c, g)] + [("RP", 3, m) for m in range(ROW_TILES)]
             if kind == "RP":

@@ -281,7 +281,7 @@ def tile_attention_pa_kernel(
         ]
         for c in range(2, VALUES):
             v_list += [("RP", c - 2, m) for m in range(ROW_TILES)]
-            v_list += [("EV", c, (3, 1)), ("IV", c, 0), ("RA", c - 2, 3), ("IV", c, 1)]
+            v_list += [("EV", c, (2, 1)), ("IV", c, 0), ("RA", c - 2, 3), ("IV", c, 1)]
             v_list += [("Q", c, g) for g in range(PASSES)]
         v_list += [("RP", 3, m) for m in range(ROW_TILES)]
         v_list += [("Q", VALUES, 0), ("RA", 3, 3), ("Q", VALUES, 1), ("Q", VALUES, 2), ("Q", VALUES, 3)]
@@ -297,7 +297,7 @@ def tile_attention_pa_kernel(
         s_list += [("E", 1, (3, 0)), ("E", 1, (3, 1))]
         for c in range(2, VALUES):
             s_list += [("W", c, g) for g in (2, 3, 0, 1)]
-            s_list += [("E", c, (2, 0)), ("E", c, (2, 1)), ("E", c, (3, 0))]
+            s_list += [("E", c, (2, 0)), ("E", c, (3, 0)), ("E", c, (3, 1))]
         s_list += [("IS", VALUES, g) for g in ON_SCALAR[VALUES]]
         for m in range(ROW_TILES):
             s_list.append(("VE", 5, m))
@@ -311,7 +311,7 @@ def tile_attention_pa_kernel(
             t_list += [("IL", c + 1, g) for g in ON_TENSOR[c + 1]] + [("MT", c, m) for m in range(ROW_TILES)]
         t_list += [("MP", VALUES, g) for g in range(PASSES)]
 
-        lists = [s_list, v_list, t_list, g_list]
+        lists = [s_list, v_list, g_list, t_list]
         steps = set(s_list + v_list + t_list + g_list)
 
         def empties(c, g):
@@ -402,7 +402,7 @@ def tile_attention_pa_kernel(
         while any(at[i] < len(lists[i]) for i in range(4)):
             moved = False
             for i in range(4):
-                while at[i] < len(lists[i]) and all(n in done for n in needs(lists[i][at[i]])):
+                if at[i] < len(lists[i]) and all(n in done for n in needs(lists[i][at[i]])):
                     kind, c, g = lists[i][at[i]]
                     emitters[kind](c, g)
                     done.add(lists[i][at[i]])

from contextlib import ExitStack

import concourse.mybir as mybir
from concourse.masks import make_identity

F32 = mybir.dt.float32
BF16 = mybir.dt.bfloat16
U32 = mybir.dt.uint32
U8 = mybir.dt.uint8
FP8 = mybir.dt.float8_e4m3fn
FP8X4 = mybir.dt.float8_e4m3fn_x4
MULT = mybir.AluOpType.mult
ADD = mybir.AluOpType.add
COPY = mybir.ActivationFunctionType.Copy

P = 128
PACK = 4
TOKENS = 512
DIM = 2048
PASSES = 4
NCH = 512
ROW_TILES = 4
HD = 128
HEADS = NCH // HD
CHUNKS = 6
KEYS = 0
VALUES = 5

FLOPS = 2 * TOKENS * DIM * (2048 + 512 + 512)

X_BANKS = (0, 2, 6, 0)

ON_TENSOR = {0: (), 1: (3,), 2: (2, 3), 3: (2, 3), 4: (2, 3), 5: ()}
ON_SCALAR = {0: (), 1: (), 2: (), 3: (), 4: (), 5: (0, 1, 2, 3)}


def tile_attention_pa_kernel(
    tc, x, wq_bytes, wq_scale, wk, wv, freqs_cos, freqs_sin, out_0, out_1, out_2
):
    nc = tc.nc
    x_rows = x[0].rearrange("(p m) k -> m p k", m=ROW_TILES)
    wq_view = wq_bytes.rearrange("(g p t) n -> g p t n", p=P, t=PACK)
    wk_view = wk.rearrange("(g p t) n -> g p t n", p=P, t=PACK)
    wv_view = wv.rearrange("(g p t) n -> g p t n", p=P, t=PACK)
    q_out = out_0[0].rearrange("(p m) h d -> m p (h d)", m=ROW_TILES)
    k_out = out_1[0].rearrange("(p m) h d -> m p (h d)", m=ROW_TILES)
    v_out = out_2[0].rearrange("(p m) h d -> m p (h d)", m=ROW_TILES)

    with ExitStack() as ctx:
        const = ctx.enter_context(tc.tile_pool(name="const", bufs=1))
        raw = ctx.enter_context(tc.tile_pool(name="raw", bufs=1))
        keep = ctx.enter_context(tc.tile_pool(name="keep", bufs=1))
        work = ctx.enter_context(tc.tile_pool(name="work", bufs=1))
        psum = ctx.enter_context(tc.psum_pool(name="psum", bufs=1))
        ctx.enter_context(tc.manual_schedule())

        wsc = const.tile([P, PASSES, PACK], F32, name="wsc", tag="wsc")
        nc.scalar.dma_start(out=wsc[:], in_=wq_scale.rearrange("(g p t) o -> p g (t o)", p=P, t=PACK))

        wq_b = {}
        wkv_raw = {}
        x_raw = {}

        def load_wq(c, g):
            t = raw.tile([P, PACK, NCH], U8, name="wqb%d_%d" % (c, g), tag="wqb%d_%d" % (c, g))
            nc.sync.dma_start(out=t[:], in_=wq_view[g, :, :, (c - 1) * NCH : c * NCH])
            wq_b[(c, g)] = t

        def load_kv(c, g):
            view = wk_view if c == KEYS else wv_view
            t = raw.tile([P, PACK, NCH], BF16, name="wkv%d_%d" % (c, g), tag="wkv%d_%d" % (c, g))
            nc.sync.dma_start(out=t[:], in_=view[g])
            wkv_raw[(c, g)] = t

        def load_x(m):
            x_raw[m] = work.tile([P, DIM], BF16, name="xraw%d" % m, tag="pl%d" % (4 + m))
            nc.sync.dma_start(out=x_raw[m][:], in_=x_rows[m])

        for i, g in enumerate((3, 0, 1, 2)):
            load_wq(1, g)
            load_kv(KEYS, i)
        for m in range(ROW_TILES):
            load_x(m)
        angles = const.tile([P, 4, ROW_TILES * HD // 2], BF16, name="angles", tag="angles")
        cos_rows = freqs_cos.rearrange("(p m) i -> p (m i)", m=ROW_TILES)
        sin_rows = freqs_sin.rearrange("(p m) i -> p (m i)", m=ROW_TILES)
        nc.sync.dma_start(out=angles[:, 0, :], in_=cos_rows)
        nc.sync.dma_start(out=angles[:, 3, :], in_=cos_rows)
        nc.sync.dma_start(out=angles[:, 1, :], in_=sin_rows)
        for g in range(PASSES):
            load_wq(2, g)
        for g in range(PASSES):
            load_wq(3, g)
        for g in range(PASSES):
            load_kv(VALUES, g)
        for g in range(PASSES):
            load_wq(4, g)

        ident = const.tile([P, P], F32, name="ident", tag="ident")
        make_identity(nc, ident[:])
        ident_bf = const.tile([P, P], BF16, name="ident_bf", tag="ident_bf")
        make_identity(nc, ident_bf[:])
        warm = const.tile([P, 2], F32, name="warm", tag="warm")
        nc.vector.memset(warm[:, 0:1], 0.0)
        nc.scalar.activation(out=warm[:, 1:2], in_=warm[:, 0:1], func=COPY)
        table = const.tile([P, 2, ROW_TILES, HD], F32, name="table", tag="table")

        x_codes = keep.tile([P, ROW_TILES, PASSES * P], U32, name="x_codes", tag="x_codes", align_bytes=64)
        x_scales = keep.tile([P, ROW_TILES, PASSES * P], U8, name="x_scales", tag="x_scales", align_bytes=64)
        w_codes = {}
        w_scales = {}
        planes = {}
        grouped = {}
        x_banks = {}
        x_grouped = {}
        il_banks = {}
        acc = {}
        both = {}
        tensor_passes = [(c, g) for c in range(CHUNKS) for g in ON_TENSOR[c]]

        def deferred(c, m):
            return m == 2 and c <= 3

        def widened(c):
            return KEYS < c < VALUES

        def minus_sin():
            nc.vector.tensor_scalar_mul(out=angles[:, 2, :], in0=angles[:, 1, :], scalar1=-1.0)

        def sin_table():
            nc.vector.tensor_copy(
                out=table[:].rearrange("p a m (i e) -> p a (m i) e", e=2),
                in_=angles[:].rearrange("p (a e) x -> p a x e", e=2),
            )

        def transpose_x(m):
            words = x_raw[m][:].bitcast(F32)
            for h in range(2):
                bank = psum.tile([P, 512], F32, name="xt%d_%d" % (m, h), tag="b%d" % (X_BANKS[m] + h))
                for gl in range(2):
                    g = 2 * h + gl
                    for u in range(2):
                        col = (2 * gl + u) * P
                        nc.tensor.transpose(bank[:, col : col + P], words[:, 256 * g + u : 256 * (g + 1) : 2], ident[:])
                x_banks[(m, h)] = bank

        def copy_x(m):
            x_grouped[m] = work.tile([P, DIM], BF16, name="xg%d" % m, tag="xg%d" % m, align_bytes=64)
            xg_words = x_grouped[m][:].bitcast(F32)
            for h in range(2):
                nc.scalar.copy(
                    out=xg_words[:, 512 * h : 512 * (h + 1)].rearrange("p (g r u) -> p g r u", g=2, u=2),
                    in_=x_banks[(m, h)][:].rearrange("p (g u r) -> p g r u", g=2, u=2),
                )

        def quantize_x(m):
            nc.vector.quantize_mx(out=x_codes[:, m, :].bitcast(FP8X4), scales=x_scales[:, m, :], in_=x_grouped[m][:])

        def widen(c, g):
            planes[(c, g)] = work.tile(
                [P, PACK, NCH], BF16, name="pl%d_%d" % (c, g), tag="pl%d" % ((4 * (c - 1) + g) % 8)
            )
            for t in range(PACK):
                nc.scalar.activation(
                    out=planes[(c, g)][:, t, :],
                    in_=wq_b[(c, g)][:, t, :].bitcast(FP8),
                    func=COPY,
                    scale=wsc[:, g, t : t + 1],
                )

        def source(c, g):
            return planes[(c, g)] if widened(c) else wkv_raw[(c, g)]

        def new_grouped(c, g):
            if (c, g) not in grouped:
                grouped[(c, g)] = work.tile(
                    [P, PACK * NCH], BF16, name="gr%d_%d" % (c, g), tag="gr%d" % ((4 * c + g) % 8), align_bytes=64
                )
            return grouped[(c, g)]

        def interleave(eng_copy, c, g):
            eng_copy(
                out=new_grouped(c, g)[:].rearrange("p (c i t) -> p c t i", i=4, t=PACK),
                in_=source(c, g)[:].rearrange("p t (c i) -> p c t i", i=4),
            )

        def tensor_interleave(c, g):
            pair = tensor_passes.index((c, g)) % 2
            src = source(c, g)
            for h in range(2):
                bank = psum.tile([P, 2 * NCH], BF16, name="il%d_%d_%d" % (c, g, h), tag="b%d" % (4 + 2 * pair + h))
                for q in range(2):
                    n0 = (2 * h + q) * P
                    nc.tensor.matmul(
                        out=bank[:, q * NCH : (q + 1) * NCH],
                        lhsT=ident_bf[:],
                        rhs=src[:, :, n0 : n0 + P].rearrange("p t n -> p n t"),
                        start=True,
                        stop=True,
                    )
                il_banks[(c, g, h)] = bank

        def evacuate(eng_copy, c, g, h):
            words = new_grouped(c, g)[:].bitcast(F32)
            eng_copy(out=words[:, h * NCH : (h + 1) * NCH], in_=il_banks[(c, g, h)][:].bitcast(F32))

        def quantize_w(c, g):
            if c not in w_codes:
                w_codes[c] = keep.tile(
                    [P, PASSES, NCH], U32, name="w_codes%d" % c, tag="w_codes%d" % (c % 3), align_bytes=64
                )
                w_scales[c] = keep.tile(
                    [P, PASSES, NCH], U8, name="w_scales%d" % c, tag="w_scales%d" % (c % 3), align_bytes=64
                )
            nc.vector.quantize_mx(
                out=w_codes[c][:, g, :].bitcast(FP8X4), scales=w_scales[c][:, g, :], in_=grouped[(c, g)][:]
            )

        def one_matmul(c, m, g, first, last):
            if first:
                acc[(c, m)] = psum.tile([P, NCH], F32, name="acc%d_%d" % (c, m), tag="b%d" % (4 + m if c == 4 else m))
            nc.tensor.matmul_mx(
                out=acc[(c, m)][:],
                lhsT=x_codes[:, m, g * P : (g + 1) * P].bitcast(FP8X4),
                lhsT_scale=x_scales[:, m, g * P : (g + 1) * P],
                rhs=w_codes[c][:, g, :].bitcast(FP8X4),
                rhs_scale=w_scales[c][:, g, :],
                start=first,
                stop=last,
            )

        def multiply_tile(c, m):
            for g in range(PASSES):
                one_matmul(c, m, g, g == 0, g == PASSES - 1)

        def multiply_pass(c, g):
            for m in range(ROW_TILES):
                one_matmul(c, m, g, g == 0, g == PASSES - 1)

        def store(queue, c, m, tile_ap):
            if c == KEYS:
                dst = k_out[m]
            elif c == VALUES:
                dst = v_out[m]
            else:
                dst = q_out[m, :, (c - 1) * NCH : c * NCH]
            queue.dma_start(out=dst, in_=tile_ap)

        def products(c, m):
            both[(c, m)] = work.tile([P, 2, NCH], F32, name="both%d_%d" % (c, m), tag="both%d" % m)
            shape = [P, 2, HEADS, HD // 2, 2]
            nc.vector.tensor_tensor(
                out=both[(c, m)][:].rearrange("p a (h i f) -> p a h i f", h=HEADS, f=2),
                in0=acc[(c, m)][:].rearrange("p (h i a) -> p a h i", h=HEADS, a=2).unsqueeze(4).to_broadcast(shape),
                in1=table[:, :, m, :].rearrange("p a (i f) -> p a i f", f=2).unsqueeze(2).to_broadcast(shape),
                op=MULT,
            )

        def add(eng, c, m):
            tag = "gr%d" % ((4 * c + 3) % 8) if deferred(c, m) else "r%d_%d" % (m, c % 2)
            if deferred(c, m):
                r = work.tile([P, NCH], F32, name="r%d_%d" % (c, m), tag=tag, align_bytes=64)
            else:
                r = work.tile([P, NCH], F32, name="r%d_%d" % (c, m), tag=tag)
            eng.tensor_tensor(out=r[:], in0=both[(c, m)][:, 0, :], in1=both[(c, m)][:, 1, :], op=ADD)
            store(nc.sync, c, m, r[:])

        v_rows = {}

        def copy_v(m):
            v_rows[m] = work.tile([P, NCH], F32, name="rv%d" % m, tag="rv%d" % m)
            nc.scalar.copy(out=v_rows[m][:], in_=acc[(VALUES, m)][:])

        def store_v(m):
            store(nc.scalar, VALUES, m, v_rows[m][:])

        v_list = [
            ("IV", 0, 0), ("IV", 0, 1), ("Q", 0, 0), ("IV", 0, 2), ("Q", 0, 1), ("IV", 0, 3), ("Q", 0, 2), ("Q", 0, 3),
            ("IV", 1, 0), ("QX", 0, 0), ("IV", 1, 1), ("QX", 0, 1), ("Q", 1, 0), ("QX", 0, 2), ("IV", 1, 2), ("QX", 0, 3),
            ("NEG", 0, 0), ("Q", 1, 1), ("Q", 1, 2), ("SIN", 0, 0), ("Q", 1, 3),
        ]
        for c in range(2, VALUES):
            v_list += [("RP", c - 2, m) for m in range(ROW_TILES)]
            v_list += [("EV", c, (2, 1)), ("IV", c, 0), ("RA", c - 2, 3), ("IV", c, 1)]
            v_list += [("Q", c, g) for g in range(PASSES)]
        v_list += [("RP", 3, m) for m in range(ROW_TILES)]
        v_list += [("Q", VALUES, 0), ("RA", 3, 3), ("Q", VALUES, 1), ("Q", VALUES, 2), ("Q", VALUES, 3)]
        v_list += [("RP", 4, m) for m in range(ROW_TILES)] + [("RA", 4, 2), ("RA", 4, 3)]

        g_list = []
        for c in range(5):
            if c > 0:
                g_list.append(("GA", c - 1, 2))
            g_list += [("GA", c, 0), ("GA", c, 1)]

        s_list = [("W", 1, g) for g in (3, 0, 1, 2)] + [("XE", 0, m) for m in range(ROW_TILES)]
        s_list += [("E", 1, (3, 0)), ("E", 1, (3, 1))]
        for c in range(2, VALUES):
            s_list += [("W", c, g) for g in (2, 3, 0, 1)]
            s_list += [("E", c, (2, 0)), ("E", c, (3, 0)), ("E", c, (3, 1))]
        s_list += [("IS", VALUES, g) for g in ON_SCALAR[VALUES]]
        for m in range(ROW_TILES):
            s_list.append(("VE", 5, m))
            if m > 0:
                s_list.append(("VS", 5, m - 1))
        s_list.append(("VS", 5, ROW_TILES - 1))

        t_list = [("IL", 1, g) for g in ON_TENSOR[1]] + [("TX", 0, m) for m in range(ROW_TILES)]
        t_list += [("MT", 0, m) for m in range(ROW_TILES)]
        for c in range(1, VALUES):
            t_list += [("IL", c + 1, g) for g in ON_TENSOR[c + 1]] + [("MT", c, m) for m in range(ROW_TILES)]
        t_list += [("MP", VALUES, g) for g in range(PASSES)]

        lists = [s_list, v_list, g_list, t_list]
        steps = set(s_list + v_list + t_list + g_list)

        def empties(c, g):
            return [(k, c, (g, h)) for h in range(2) for k in ("E", "EV") if (k, c, (g, h)) in steps]

        def interleaver(c, g):
            if g in ON_TENSOR[c]:
                return ("IL", c, g)
            return ("IS" if g in ON_SCALAR[c] else "IV", c, g)

        def needs(step):
            kind, c, g = step
            out = []
            if kind == "W":
                if c == 2:
                    out.append(("TX", 0, g))
                elif c > 2:
                    out.append(interleaver(c - 2, g))
            if kind in ("IV", "IS", "IL") and widened(c):
                out.append(("W", c, g))
            if kind in ("IV", "IS", "E", "EV"):
                p = g[0] if kind in ("E", "EV") else g
                if c >= 2:
                    out.append(("Q", c - 2, p))
                if c >= 4 and p == 3:
                    out.append(("GA", c - 4, 2))
            if kind in ("E", "EV"):
                out.append(("IL", c, g[0]))
            if kind == "IL":
                k = tensor_passes.index((c, g))
                out += ([], [("XE", 0, 2)])[k] if k < 2 else empties(tensor_passes[k - 2][0], tensor_passes[k - 2][1])
            if kind == "Q":
                out += empties(c, g) if g in ON_TENSOR[c] else [interleaver(c, g)]
                if c >= 3:
                    out.append(("MT", c - 3, ROW_TILES - 1))
            if kind == "TX" and g == 3:
                out.append(("XE", 0, 0))
            if kind == "XE":
                out.append(("TX", 0, g))
            if kind == "QX":
                out.append(("XE", 0, g))
            if kind == "MT":
                out += [("Q", c, p) for p in range(PASSES)] + [("QX", 0, g)]
                if c == 4:
                    out += empties(4, 2) + empties(4, 3)
                else:
                    out.append(("XE", 0, (3, 3, 1, 1)[g]) if c == 0 else ("RP", c - 1, g))
            if kind == "MP":
                out += [("Q", c, g)] + [("RP", 3, m) for m in range(ROW_TILES)]
            if kind == "RP":
                out += [("MT", c, g), ("SIN", 0, 0)]
                if c > 0:
                    out.append(("GA" if ("GA", c - 1, g) in steps else "RA", c - 1, g))
            if kind in ("RA", "GA"):
                out.append(("RP", c, g))
                if deferred(c, g):
                    out.append(("Q", c + 2, 3))
            if kind == "VE":
                out.append(("MP", VALUES, PASSES - 1))
            if kind == "SIN":
                out.append(("NEG", 0, 0))
            return out

        emitters = {
            "W": widen,
            "IV": lambda c, g: interleave(nc.vector.tensor_copy, c, g),
            "IS": lambda c, g: interleave(nc.scalar.copy, c, g),
            "IL": tensor_interleave,
            "E": lambda c, g: evacuate(nc.scalar.copy, c, g[0], g[1]),
            "EV": lambda c, g: evacuate(nc.vector.tensor_copy, c, g[0], g[1]),
            "Q": quantize_w,
            "TX": lambda c, m: transpose_x(m),
            "XE": lambda c, m: copy_x(m),
            "QX": lambda c, m: quantize_x(m),
            "MT": multiply_tile,
            "MP": multiply_pass,
            "RP": products,
            "RA": lambda c, m: add(nc.vector, c, m),
            "GA": lambda c, m: add(nc.gpsimd, c, m),
            "VE": lambda c, m: copy_v(m),
            "VS": lambda c, m: store_v(m),
            "NEG": lambda c, m: minus_sin(),
            "SIN": lambda c, m: sin_table(),
        }

        at = [0, 0, 0, 0]
        done = set()
        while any(at[i] < len(lists[i]) for i in range(4)):
            moved = False
            for i in range(4):
                if at[i] < len(lists[i]) and all(n in done for n in needs(lists[i][at[i]])):
                    kind, c, g = lists[i][at[i]]
                    emitters[kind](c, g)
                    done.add(lists[i][at[i]])
                    at[i] += 1
                    moved = True
            assert moved, "the four orders wait for each other"
